import numpy as np
import ml_dtypes


def mxq(x, axis, fmt="e4m3"):
    dtype, down = {"e4m3": (ml_dtypes.float8_e4m3fn, 7), "e5m2": (ml_dtypes.float8_e5m2, 14)}[fmt]
    v = np.moveaxis(np.asarray(x, np.float32).astype(ml_dtypes.bfloat16).astype(np.float64), axis, -1)
    blocks = v.reshape(v.shape[:-1] + (-1, 32))
    amax = np.abs(blocks).max(-1, keepdims=True)
    byte = np.maximum(np.where(amax > 0, np.frexp(amax)[1] - 1 + 127, 0) - down, 1)
    scale = np.exp2(byte - 127.0)
    codes = (blocks / scale).astype(np.float32).astype(dtype).astype(np.float64)
    return np.moveaxis((codes * scale).reshape(v.shape), -1, axis)


WIDE = False


def mx_kscale(k):
    if not WIDE:
        return np.ones(k)
    levels = np.array([10, -10, 5, -5, 0])
    a = np.random.permutation(np.resize(levels, k // 512 * 4)).reshape(k // 512, 4)
    idx = np.arange(k)
    return np.exp2(a[idx // 512, idx % 128 // 32])


BF16 = ml_dtypes.bfloat16


def bf(x):
    return np.asarray(x, np.float32).astype(BF16)


def f64(x):
    return np.asarray(x).astype(np.float64)


E2M1 = np.array([0.0, 0.5, 1.0, 1.5, 2.0, 3.0, 4.0, 6.0, -0.0, -0.5, -1.0, -1.5, -2.0, -3.0, -4.0, -6.0])


def pack_weight(w, fmt):
    k, n = w.shape
    w = f64(bf(w)).reshape(k // 32, 32, n)
    amax = np.abs(w).max(1)
    if fmt == "e4m3":
        byte = np.frexp(amax)[1] - 1 + 127 - 7
    else:
        mant, ex = np.frexp(amax / 6.0)
        byte = np.where(mant > 0.5, ex, ex - 1) + 127
    byte = np.clip(np.where(amax > 0, byte, 1), 1, 254)
    scaled = (w * np.exp2(127.0 - byte)[:, None, :]).reshape(k, n).astype(np.float32)
    by_word = np.ascontiguousarray(scaled.reshape(k // 512, 128, 4, n).transpose(0, 1, 3, 2))
    if fmt == "e4m3":
        words = by_word.astype(ml_dtypes.float8_e4m3fn).view(np.uint8)
    else:
        c = by_word.astype(ml_dtypes.float4_e2m1fn).view(np.uint8) & 0xF
        words = c[..., 0::2] | (c[..., 1::2] << 4)
    return np.ascontiguousarray(words), np.ascontiguousarray(byte.astype(np.uint8).reshape(k // 512, 16, n))


def unpack_weight(words, scales, fmt):
    g, p, n, _ = words.shape
    if fmt == "e4m3":
        vals = np.ascontiguousarray(words).view(ml_dtypes.float8_e4m3fn).astype(np.float64)
    else:
        nib = np.empty((g, p, n, 4), np.uint8)
        nib[..., 0::2] = words & 0xF
        nib[..., 1::2] = words >> 4
        vals = E2M1[nib]
    vals = vals * np.repeat(np.exp2(scales.astype(np.float64) - 127.0), 8, axis=1)[..., None]
    return vals.transpose(0, 1, 3, 2).reshape(g * 512, n)


B, T, H, W, C, NH, RD = 2, 4, 8, 16, 1024, 16, 16
N = T * H * W
HD = C // NH
ROT = 3 * RD
MAX_FREQ = 256.0


def axis_freqs(n):
    base = np.linspace(1.0, MAX_FREQ / 2.0, RD // 2) * np.pi
    pos = np.linspace(-1.0, 1.0, n)
    return np.repeat(pos[:, None] * base[None, :], 2, axis=-1)


def axial_freqs():
    ft = np.broadcast_to(axis_freqs(T)[:, None, None, :], (T, H, W, RD))
    fh = np.broadcast_to(axis_freqs(H)[None, :, None, :], (T, H, W, RD))
    fw = np.broadcast_to(axis_freqs(W)[None, None, :, :], (T, H, W, RD))
    return np.concatenate([ft, fh, fw], axis=-1)


def rotate_half(v):
    p = v.reshape(*v.shape[:-1], -1, 2)
    return np.stack([-p[..., 1], p[..., 0]], axis=-1).reshape(v.shape)


def apply_rope(freqs, t):
    tm, tr = t[..., :ROT], t[..., ROT:]
    tm = tm * np.cos(freqs) + rotate_half(tm) * np.sin(freqs)
    return np.concatenate([tm, tr], axis=-1)


def setup_inputs():
    s = mx_kscale(C)
    x = bf(np.random.standard_normal((B, N, C)) * s)
    words, scales = pack_weight(np.random.standard_normal((C, 3 * C)) * 0.6 / np.sqrt(C) / s[:, None], 'e4m3')
    return {'x': x, 'Wqkv_words': words, 'Wqkv_scales': scales}


def reference(x, Wqkv_words, Wqkv_scales):
    qkv = mxq(f64(x), 2, 'e4m3') @ unpack_weight(Wqkv_words, Wqkv_scales, 'e4m3')
    qkv = qkv.reshape(B, N, 3, NH, HD).transpose(2, 0, 3, 1, 4)
    q, k, v = qkv[0], qkv[1], qkv[2]
    freqs = axial_freqs()
    q_rot = apply_rope(freqs, q.reshape(B, NH, T, H, W, HD)).reshape(B, NH, N, HD)
    k_rot = apply_rope(freqs, k.reshape(B, NH, T, H, W, HD)).reshape(B, NH, N, HD)
    return q_rot, k_rot, v

@@ -1,0 +1,251 @@
+import math
+from contextlib import ExitStack
+
+import concourse.mybir as mybir
+from concourse.masks import make_identity
+
+F32 = mybir.dt.float32
+BF16 = mybir.dt.bfloat16
+I32 = mybir.dt.int32
+U32 = mybir.dt.uint32
+U8 = mybir.dt.uint8
+FP8X4 = mybir.dt.float8_e4m3fn_x4
+ALU = mybir.AluOpType
+ACT = mybir.ActivationFunctionType
+
+P = 128
+BATCH = 2
+TOKENS = 512
+CHANNELS = 1024
+HEADS = 16
+HEAD_DIM = 64
+GROUPS = TOKENS // P
+PACK = 4
+K_PASS = P * PACK
+PASSES = CHANNELS // K_PASS
+WORDS_PER_PASS = K_PASS // 2
+N_TILE = 512
+BLOCK_HEADS = N_TILE // HEAD_DIM
+HALVES = HEADS // BLOCK_HEADS
+COLUMNS = 3 * HEADS * HEAD_DIM
+
+AXES = 3
+FREQS = 8
+PAIRS = AXES * FREQS
+ROTATED = 2 * PAIRS
+GROUPS_PER_ADD = 2
+
+Q, K, V = 0, 1, 2
+
+FLOPS = 2 * BATCH * TOKENS * CHANNELS * COLUMNS
+
+HALF_TURN = 2 * 105 * 7
+QUARTER_TURN = HALF_TURN // 2
+ROUND_MAGIC = 1.5 * 2.0**23
+
+
+def build_rotation_tables(nc, pool):
+    partition = pool.tile([P, 1], I32)
+    nc.gpsimd.iota(partition[:], pattern=[[0, 1]], base=0, channel_multiplier=1)
+    freq7 = pool.tile([P, FREQS], I32)
+    nc.gpsimd.iota(freq7[:], pattern=[[127, FREQS]], base=7, channel_multiplier=0)
+    group14 = pool.tile([P, GROUPS], I32)
+    nc.gpsimd.iota(group14[:], pattern=[[14, GROUPS]], base=0, channel_multiplier=0)
+
+    grid = pool.tile([P, AXES], I32)
+    nc.vector.tensor_scalar(out=grid[:, 0:1], in0=partition[:], scalar1=5, scalar2=None, op0=ALU.arith_shift_right)
+    nc.vector.tensor_scalar(
+        out=grid[:, 1:2], in0=partition[:], scalar1=2, scalar2=7, op0=ALU.arith_shift_right, op1=ALU.bitwise_and
+    )
+    nc.vector.tensor_scalar(out=grid[:, 2:3], in0=partition[:], scalar1=3, scalar2=None, op0=ALU.bitwise_and)
+
+    pos105 = pool.tile([P, GROUPS, AXES], F32)
+    for axis, step in enumerate((70.0, 30.0, 56.0)):
+        nc.vector.tensor_scalar(
+            out=pos105[:, :, axis],
+            in0=grid[:, axis : axis + 1].to_broadcast([P, GROUPS]),
+            scalar1=step,
+            scalar2=-105.0,
+            op0=ALU.mult,
+            op1=ALU.add,
+        )
+    nc.vector.tensor_tensor(out=pos105[:, :, 2], in0=pos105[:, :, 2], in1=group14[:], op=ALU.add)
+
+    product = pool.tile([P, GROUPS * AXES, FREQS], F32)
+    nc.vector.tensor_tensor(
+        out=product[:],
+        in0=pos105[:].rearrange("p j a -> p (j a)").unsqueeze(2).to_broadcast([P, GROUPS * AXES, FREQS]),
+        in1=freq7[:].unsqueeze(1).to_broadcast([P, GROUPS * AXES, FREQS]),
+        op=ALU.mult,
+    )
+    width = GROUPS * PAIRS
+    units = pool.tile([P, 3, width], F32)
+    for phase in range(3):
+        nc.vector.tensor_scalar(
+            out=units[:, phase, :],
+            in0=product[:].rearrange("p r f -> p (r f)"),
+            scalar1=2.0,
+            scalar2=float(phase * QUARTER_TURN),
+            op0=ALU.mult,
+            op1=ALU.add,
+        )
+    shifted = pool.tile([P, 3, width], F32)
+    nc.vector.tensor_scalar(
+        out=shifted[:], in0=units[:], scalar1=1.0 / HALF_TURN, scalar2=ROUND_MAGIC, op0=ALU.mult, op1=ALU.add
+    )
+    half_turns = pool.tile([P, 3, width], I32)
+    nc.vector.tensor_scalar(out=half_turns[:], in0=shifted[:], scalar1=ROUND_MAGIC, scalar2=None, op0=ALU.subtract)
+    rest = pool.tile([P, 3, width], F32)
+    nc.vector.scalar_tensor_tensor(
+        out=rest[:], in0=half_turns[:], scalar=-float(HALF_TURN), in1=units[:], op0=ALU.mult, op1=ALU.add
+    )
+    odd = pool.tile([P, 3, width], I32)
+    nc.vector.tensor_scalar(out=odd[:], in0=half_turns[:], scalar1=1, scalar2=None, op0=ALU.bitwise_and)
+    sign = pool.tile([P, 3, width], F32)
+    nc.vector.tensor_scalar(out=sign[:], in0=odd[:], scalar1=-2.0, scalar2=1.0, op0=ALU.mult, op1=ALU.add)
+    sine = pool.tile([P, 3, width], F32)
+    nc.scalar.activation(out=sine[:], in_=rest[:], func=ACT.Sin, scale=math.pi / HALF_TURN)
+    tables = pool.tile([P, 3, GROUPS, PAIRS], F32)
+    nc.vector.tensor_tensor(
+        out=tables[:].rearrange("p s j i -> p s (j i)"), in0=sine[:], in1=sign[:], op=ALU.mult
+    )
+    return tables
+
+
+def tile_attention_pa_kernel(tc, x, Wqkv_words, Wqkv_scales, out_0, out_1, out_2):
+    nc = tc.nc
+    outs = (out_0, out_1, out_2)
+    with ExitStack() as ctx:
+        keep = ctx.enter_context(tc.tile_pool(name="keep", bufs=1))
+        regroup = ctx.enter_context(tc.tile_pool(name="regroup", bufs=GROUPS))
+        results = ctx.enter_context(tc.tile_pool(name="results", bufs=6))
+        crosses = ctx.enter_context(tc.tile_pool(name="crosses", bufs=4))
+        psum = ctx.enter_context(tc.psum_pool(name="psum", bufs=8))
+
+        x_rows = [keep.tile([P, GROUPS, CHANNELS], BF16, name="x_rows%d" % b) for b in range(BATCH)]
+        x_codes = keep.tile([P, BATCH, GROUPS, PASSES * P], U32, align_bytes=64)
+        x_scales = keep.tile([P, BATCH, GROUPS, PASSES * P], U8, align_bytes=64)
+        w_codes = keep.tile([P, PASSES, COLUMNS], U32, align_bytes=64)
+        w_scales = keep.tile([P, PASSES, COLUMNS], U8, align_bytes=64)
+
+        nc.vector.memset(w_scales[:].bitcast(I32), 0)
+
+        def load_x(b):
+            nc.sync.dma_start(
+                out=x_rows[b][:].rearrange("p j k -> p (j k)"),
+                in_=x[b].rearrange("(p j) k -> p (j k)", j=GROUPS),
+            )
+
+        def load_w_scales():
+            rows = Wqkv_scales.bitcast(I32).rearrange("g q n -> q g n")
+            plane = w_scales[:].bitcast(I32)
+            for quadrant in range(4):
+                nc.sync.dma_start(
+                    out=plane[32 * quadrant : 32 * quadrant + 4], in_=rows[4 * quadrant : 4 * quadrant + 4]
+                )
+
+        def block_columns(which, half):
+            first = (which * HALVES + half) * N_TILE
+            return slice(first, first + N_TILE)
+
+        def load_w_codes(which, half):
+            words = Wqkv_words.rearrange("g p n t -> g p (n t)").bitcast(I32).rearrange("g p n -> p g n")
+            cols = block_columns(which, half)
+            nc.sync.dma_start(out=w_codes[:, :, cols].bitcast(I32), in_=words[:, :, cols])
+
+        load_x(0)
+        load_w_scales()
+        load_w_codes(Q, 0)
+        load_x(1)
+        load_w_codes(V, 0)
+        load_w_codes(K, 0)
+        for which in (Q, V, K):
+            load_w_codes(which, 1)
+
+        identity = keep.tile([P, P], F32)
+        make_identity(nc, identity[:])
+        tables = build_rotation_tables(nc, keep)
+
+        def transpose_tokens(b):
+            grouped_tiles = []
+            for j in range(GROUPS):
+                words = x_rows[b][:, j, :].bitcast(F32)
+                bank = psum.tile([P, PASSES, 2, P], F32, tag="bank", name="x_bank")
+                for g in range(PASSES):
+                    for u in range(2):
+                        pass_words = slice(g * WORDS_PER_PASS + u, (g + 1) * WORDS_PER_PASS, 2)
+                        nc.tensor.transpose(bank[:, g, u, :], words[:, pass_words], identity[:])
+                grouped = regroup.tile([P, PASSES, P, PACK], BF16, align_bytes=64, name="grouped")
+                nc.scalar.copy(out=grouped[:].bitcast(F32), in_=bank[:].rearrange("p g u n -> p g n u"))
+                grouped_tiles.append(grouped)
+            return grouped_tiles
+
+        def quantise_tokens(b, grouped_tiles):
+            for j in range(GROUPS):
+                nc.vector.quantize_mx(
+                    out=x_codes[:, b, j, :].bitcast(FP8X4),
+                    scales=x_scales[:, b, j, :],
+                    in_=grouped_tiles[j][:].rearrange("p g n t -> p (g n t)"),
+                )
+
+        def project_block(b, which, half):
+            cols = block_columns(which, half)
+            staged = results.tile([P, BLOCK_HEADS, GROUPS, HEAD_DIM], F32, name="staged")
+            for first_group in range(0, GROUPS, GROUPS_PER_ADD):
+                if which != V:
+                    cross = crosses.tile([P, 2, BLOCK_HEADS, GROUPS_PER_ADD, PAIRS], F32, name="cross")
+                for j in range(first_group, first_group + GROUPS_PER_ADD):
+                    acc = psum.tile([P, BLOCK_HEADS, HEAD_DIM], F32, tag="bank", name="acc")
+                    for g in range(PASSES):
+                        tokens = slice(g * P, (g + 1) * P)
+                        nc.tensor.matmul_mx(
+                            out=acc[:].rearrange("p h d -> p (h d)"),
+                            lhsT=x_codes[:, b, j, tokens].bitcast(FP8X4),
+                            lhsT_scale=x_scales[:, b, j, tokens],
+                            rhs=w_codes[:, g, cols].bitcast(FP8X4),
+                            rhs_scale=w_scales[:, g, cols],
+                            start=(g == 0),
+                            stop=(g == PASSES - 1),
+                        )
+                    if which == V:
+                        nc.scalar.copy(out=staged[:, :, j, :], in_=acc[:])
+                        continue
+                    nc.scalar.copy(out=staged[:, :, j, ROTATED:], in_=acc[:, :, ROTATED:])
+                    pairs = acc[:, :, :ROTATED].rearrange("p h (i e) -> p h i e", e=2)
+                    shape = [P, BLOCK_HEADS, PAIRS, 2]
+                    nc.vector.tensor_tensor(
+                        out=staged[:, :, j, :ROTATED].rearrange("p h (i e) -> p h i e", e=2),
+                        in0=pairs,
+                        in1=tables[:, 1, j, :].unsqueeze(1).unsqueeze(3).to_broadcast(shape),
+                        op=ALU.mult,
+                    )
+                    for e in range(2):
+                        nc.vector.tensor_tensor(
+                            out=cross[:, e, :, j - first_group, :],
+                            in0=pairs[:, :, :, 1 - e],
+                            in1=tables[:, 2 - 2 * e, j, :].unsqueeze(1).to_broadcast(shape[:3]),
+                            op=ALU.mult,
+                        )
+                if which != V:
+                    some = slice(first_group, first_group + GROUPS_PER_ADD)
+                    target = staged[:, :, some, :ROTATED].rearrange("p h j (i e) -> p h j i e", e=2)
+                    nc.gpsimd.tensor_tensor(
+                        out=target, in0=target, in1=cross[:].rearrange("p e h j i -> p h j i e"), op=ALU.add
+                    )
+            heads = slice(half * BLOCK_HEADS, (half + 1) * BLOCK_HEADS)
+            nc.sync.dma_start(
+                out=outs[which][b, heads].rearrange("h (p j) d -> p h (j d)", j=GROUPS),
+                in_=staged[:].rearrange("p h j d -> p h (j d)"),
+            )
+
+        quantise_tokens(0, transpose_tokens(0))
+        project_block(0, Q, 0)
+        grouped_1 = transpose_tokens(1)
+        project_block(0, V, 0)
+        project_block(0, K, 0)
+        quantise_tokens(1, grouped_1)
+        for which in (Q, V, K):
+            project_block(1, which, 0)
+        for b in range(BATCH):
+            for which in (Q, V, K):
+                project_block(b, which, 1)

@@ -105,11 +105,23 @@ def build_rotation_tables(nc, pool):
     nc.vector.tensor_scalar(out=sign[:], in0=odd[:], scalar1=-2.0, scalar2=1.0, op0=ALU.mult, op1=ALU.add)
     sine = pool.tile([P, 3, width], F32)
     nc.scalar.activation(out=sine[:], in_=rest[:], func=ACT.Sin, scale=math.pi / HALF_TURN)
-    tables = pool.tile([P, 3, GROUPS, PAIRS], F32)
+    cosines = pool.tile([P, GROUPS, ROTATED], F32)
     nc.vector.tensor_tensor(
-        out=tables[:].rearrange("p s j i -> p s (j i)"), in0=sine[:], in1=sign[:], op=ALU.mult
+        out=cosines[:].rearrange("p j (i e) -> p (j i) e", e=2),
+        in0=sine[:, 1, :].unsqueeze(2).to_broadcast([P, width, 2]),
+        in1=sign[:, 1, :].unsqueeze(2).to_broadcast([P, width, 2]),
+        op=ALU.mult,
     )
-    return tables
+    sines = pool.tile([P, GROUPS, ROTATED], F32)
+    for e in range(2):
+        phase = 2 - 2 * e
+        nc.vector.tensor_tensor(
+            out=sines[:].rearrange("p j (i e) -> p (j i) e", e=2)[:, :, e],
+            in0=sine[:, phase, :],
+            in1=sign[:, phase, :],
+            op=ALU.mult,
+        )
+    return cosines, sines
 
 
 def tile_attention_pa_kernel(tc, x, Wqkv_words, Wqkv_scales, out_0, out_1, out_2):
@@ -164,7 +176,7 @@ def tile_attention_pa_kernel(tc, x, Wqkv_words, Wqkv_scales, out_0, out_1, out_2
 
         identity = keep.tile([P, P], F32)
         make_identity(nc, identity[:])
-        tables = build_rotation_tables(nc, keep)
+        cosines, sines = build_rotation_tables(nc, keep)
 
         def transpose_tokens(b):
             grouped_tiles = []
@@ -193,7 +205,7 @@ def tile_attention_pa_kernel(tc, x, Wqkv_words, Wqkv_scales, out_0, out_1, out_2
             staged = results.tile([P, BLOCK_HEADS, GROUPS, HEAD_DIM], F32, name="staged")
             for first_group in range(0, GROUPS, GROUPS_PER_ADD):
                 if which != V:
-                    cross = crosses.tile([P, 2, BLOCK_HEADS, GROUPS_PER_ADD, PAIRS], F32, name="cross")
+                    cross = crosses.tile([P, BLOCK_HEADS, GROUPS_PER_ADD, ROTATED], F32, name="cross")
                 for j in range(first_group, first_group + GROUPS_PER_ADD):
                     acc = psum.tile([P, BLOCK_HEADS, HEAD_DIM], F32, tag="bank", name="acc")
                     for g in range(PASSES):
@@ -211,27 +223,23 @@ def tile_attention_pa_kernel(tc, x, Wqkv_words, Wqkv_scales, out_0, out_1, out_2
                         nc.scalar.copy(out=staged[:, :, j, :], in_=acc[:])
                         continue
                     nc.scalar.copy(out=staged[:, :, j, ROTATED:], in_=acc[:, :, ROTATED:])
-                    pairs = acc[:, :, :ROTATED].rearrange("p h (i e) -> p h i e", e=2)
-                    shape = [P, BLOCK_HEADS, PAIRS, 2]
                     nc.vector.tensor_tensor(
-                        out=staged[:, :, j, :ROTATED].rearrange("p h (i e) -> p h i e", e=2),
-                        in0=pairs,
-                        in1=tables[:, 1, j, :].unsqueeze(1).unsqueeze(3).to_broadcast(shape),
+                        out=staged[:, :, j, :ROTATED],
+                        in0=acc[:, :, :ROTATED],
+                        in1=cosines[:, j, :].unsqueeze(1).to_broadcast([P, BLOCK_HEADS, ROTATED]),
                         op=ALU.mult,
                     )
-                    for e in range(2):
-                        nc.vector.tensor_tensor(
-                            out=cross[:, e, :, j - first_group, :],
-                            in0=pairs[:, :, :, 1 - e],
-                            in1=tables[:, 2 - 2 * e, j, :].unsqueeze(1).to_broadcast(shape[:3]),
-                            op=ALU.mult,
-                        )
+                    shape = [P, BLOCK_HEADS, PAIRS, 2]
+                    nc.vector.tensor_tensor(
+                        out=cross[:, :, j - first_group, :].rearrange("p h (i e) -> p h i e", e=2),
+                        in0=acc[:, :, :ROTATED].rearrange("p h (i e) -> p h i e", e=2)[:, :, :, ::-1],
+                        in1=sines[:, j, :].rearrange("p (i e) -> p i e", e=2).unsqueeze(1).to_broadcast(shape),
+                        op=ALU.mult,
+                    )
                 if which != V:
                     some = slice(first_group, first_group + GROUPS_PER_ADD)
-                    target = staged[:, :, some, :ROTATED].rearrange("p h j (i e) -> p h j i e", e=2)
-                    nc.gpsimd.tensor_tensor(
-                        out=target, in0=target, in1=cross[:].rearrange("p e h j i -> p h j i e"), op=ALU.add
-                    )
+                    target = staged[:, :, some, :ROTATED]
+                    nc.gpsimd.tensor_tensor(out=target, in0=target, in1=cross[:], op=ALU.add)
             heads = slice(half * BLOCK_HEADS, (half + 1) * BLOCK_HEADS)
             nc.sync.dma_start(
                 out=outs[which][b, heads].rearrange("h (p j) d -> p h (j d)", j=GROUPS),

@@ -1,5 +1,6 @@
 import math
 from contextlib import ExitStack
+from functools import partial
 
 import concourse.mybir as mybir
 from concourse.masks import make_identity
@@ -19,23 +20,35 @@ TOKENS = 512
 CHANNELS = 1024
 HEADS = 16
 HEAD_DIM = 64
-GROUPS = TOKENS // P
+GROUPS = BATCH * TOKENS // P
 PACK = 4
 K_PASS = P * PACK
 PASSES = CHANNELS // K_PASS
 WORDS_PER_PASS = K_PASS // 2
-N_TILE = 512
-BLOCK_HEADS = N_TILE // HEAD_DIM
-HALVES = HEADS // BLOCK_HEADS
+BANK_HEADS = 8
 COLUMNS = 3 * HEADS * HEAD_DIM
 
 AXES = 3
 FREQS = 8
 PAIRS = AXES * FREQS
 ROTATED = 2 * PAIRS
-GROUPS_PER_ADD = 2
+SHARED_PAIRS = 2 * FREQS
+PLACES = 2 + GROUPS
 
 Q, K, V = 0, 1, 2
+
+ROTATED_BLOCKS = (
+    (Q, 0, 4, 2),
+    (Q, 4, 4, 2),
+    (K, 0, 4, 2),
+    (K, 4, 4, 2),
+    (Q, 8, 4, 2),
+    (Q, 12, 4, 2),
+    (K, 8, 4, 2),
+    (K, 12, 4, 1),
+)
+PLAIN_BLOCKS = ((V, 0, 8, 1), (V, 8, 8, 1))
+PLAIN_LEAD = 4
 
 FLOPS = 2 * BATCH * TOKENS * CHANNELS * COLUMNS
 
@@ -45,83 +58,95 @@ ROUND_MAGIC = 1.5 * 2.0**23
 
 
 def build_rotation_tables(nc, pool):
+    warm = pool.tile([P, 1], F32)
+    nc.gpsimd.memset(warm[:], 0.0)
+    nc.scalar.activation(out=warm[:], in_=warm[:], func=ACT.Sin)
+
     partition = pool.tile([P, 1], I32)
     nc.gpsimd.iota(partition[:], pattern=[[0, 1]], base=0, channel_multiplier=1)
-    freq7 = pool.tile([P, FREQS], I32)
-    nc.gpsimd.iota(freq7[:], pattern=[[127, FREQS]], base=7, channel_multiplier=0)
-    group14 = pool.tile([P, GROUPS], I32)
-    nc.gpsimd.iota(group14[:], pattern=[[14, GROUPS]], base=0, channel_multiplier=0)
+    group = pool.tile([P, GROUPS], I32)
+    nc.gpsimd.iota(group[:], pattern=[[1, GROUPS]], base=0, channel_multiplier=0)
+    slope = pool.tile([P, PLACES, FREQS], I32)
+    for step, places in ((70, slice(0, 1)), (30, slice(1, 2)), (14, slice(2, PLACES))):
+        nc.gpsimd.iota(
+            slope[:, places, :],
+            pattern=[[0, places.stop - places.start], [2 * step * 127, FREQS]],
+            base=2 * step * 7,
+            channel_multiplier=0,
+        )
+    start = pool.tile([P, 2, 2, FREQS], I32)
+    nc.gpsimd.iota(
+        start[:, 0], pattern=[[0, 2], [-210 * 127, FREQS]], base=QUARTER_TURN - 210 * 7, channel_multiplier=0
+    )
+    nc.gpsimd.iota(
+        start[:, 1], pattern=[[-HALF_TURN, 2], [-210 * 127, FREQS]], base=HALF_TURN - 210 * 7, channel_multiplier=0
+    )
 
     grid = pool.tile([P, AXES], I32)
     nc.vector.tensor_scalar(out=grid[:, 0:1], in0=partition[:], scalar1=5, scalar2=None, op0=ALU.arith_shift_right)
     nc.vector.tensor_scalar(
         out=grid[:, 1:2], in0=partition[:], scalar1=2, scalar2=7, op0=ALU.arith_shift_right, op1=ALU.bitwise_and
     )
-    nc.vector.tensor_scalar(out=grid[:, 2:3], in0=partition[:], scalar1=3, scalar2=None, op0=ALU.bitwise_and)
-
-    pos105 = pool.tile([P, GROUPS, AXES], F32)
-    for axis, step in enumerate((70.0, 30.0, 56.0)):
-        nc.vector.tensor_scalar(
-            out=pos105[:, :, axis],
-            in0=grid[:, axis : axis + 1].to_broadcast([P, GROUPS]),
-            scalar1=step,
-            scalar2=-105.0,
-            op0=ALU.mult,
-            op1=ALU.add,
-        )
-    nc.vector.tensor_tensor(out=pos105[:, :, 2], in0=pos105[:, :, 2], in1=group14[:], op=ALU.add)
-
-    product = pool.tile([P, GROUPS * AXES, FREQS], F32)
-    nc.vector.tensor_tensor(
-        out=product[:],
-        in0=pos105[:].rearrange("p j a -> p (j a)").unsqueeze(2).to_broadcast([P, GROUPS * AXES, FREQS]),
-        in1=freq7[:].unsqueeze(1).to_broadcast([P, GROUPS * AXES, FREQS]),
-        op=ALU.mult,
-    )
-    width = GROUPS * PAIRS
-    units = pool.tile([P, 3, width], F32)
-    for phase in range(3):
-        nc.vector.tensor_scalar(
-            out=units[:, phase, :],
-            in0=product[:].rearrange("p r f -> p (r f)"),
-            scalar1=2.0,
-            scalar2=float(phase * QUARTER_TURN),
-            op0=ALU.mult,
-            op1=ALU.add,
-        )
-    shifted = pool.tile([P, 3, width], F32)
     nc.vector.tensor_scalar(
-        out=shifted[:], in0=units[:], scalar1=1.0 / HALF_TURN, scalar2=ROUND_MAGIC, op0=ALU.mult, op1=ALU.add
+        out=grid[:, 2:3], in0=partition[:], scalar1=2, scalar2=8, op0=ALU.logical_shift_left, op1=ALU.bitwise_and
     )
-    half_turns = pool.tile([P, 3, width], I32)
-    nc.vector.tensor_scalar(out=half_turns[:], in0=shifted[:], scalar1=ROUND_MAGIC, scalar2=None, op0=ALU.subtract)
-    rest = pool.tile([P, 3, width], F32)
-    nc.vector.scalar_tensor_tensor(
-        out=rest[:], in0=half_turns[:], scalar=-float(HALF_TURN), in1=units[:], op0=ALU.mult, op1=ALU.add
-    )
-    odd = pool.tile([P, 3, width], I32)
-    nc.vector.tensor_scalar(out=odd[:], in0=half_turns[:], scalar1=1, scalar2=None, op0=ALU.bitwise_and)
-    sign = pool.tile([P, 3, width], F32)
-    nc.vector.tensor_scalar(out=sign[:], in0=odd[:], scalar1=-2.0, scalar2=1.0, op0=ALU.mult, op1=ALU.add)
-    sine = pool.tile([P, 3, width], F32)
-    nc.scalar.activation(out=sine[:], in_=rest[:], func=ACT.Sin, scale=math.pi / HALF_TURN)
-    cosines = pool.tile([P, GROUPS, ROTATED], F32)
+    column = pool.tile([P, GROUPS], F32)
+    nc.vector.tensor_tensor(out=column[:], in0=group[:], in1=grid[:, 2:3].to_broadcast([P, GROUPS]), op=ALU.add)
+
+    width = PLACES * FREQS
+    product = pool.tile([P, PLACES, FREQS], F32)
     nc.vector.tensor_tensor(
-        out=cosines[:].rearrange("p j (i e) -> p (j i) e", e=2),
-        in0=sine[:, 1, :].unsqueeze(2).to_broadcast([P, width, 2]),
-        in1=sign[:, 1, :].unsqueeze(2).to_broadcast([P, width, 2]),
+        out=product[:, :2, :], in0=grid[:, :2].unsqueeze(2).to_broadcast([P, 2, FREQS]), in1=slope[:, :2, :], op=ALU.mult
+    )
+    nc.vector.tensor_tensor(
+        out=product[:, 2:, :],
+        in0=column[:].unsqueeze(2).to_broadcast([P, GROUPS, FREQS]),
+        in1=slope[:, 2:, :],
         op=ALU.mult,
     )
-    sines = pool.tile([P, GROUPS, ROTATED], F32)
-    for e in range(2):
-        phase = 2 - 2 * e
+    units = pool.tile([P, 4, PLACES, FREQS], F32)
+    nc.vector.tensor_tensor(
+        out=units[:],
+        in0=product[:].unsqueeze(1).to_broadcast([P, 4, PLACES, FREQS]),
+        in1=start[:].rearrange("p c e f -> p (c e) f").unsqueeze(2).to_broadcast([P, 4, PLACES, FREQS]),
+        op=ALU.add,
+    )
+    flat = units[:].rearrange("p s r f -> p s (r f)")
+    shifted = pool.tile([P, 4, width], F32)
+    nc.vector.tensor_scalar(
+        out=shifted[:], in0=flat, scalar1=1.0 / HALF_TURN, scalar2=ROUND_MAGIC, op0=ALU.mult, op1=ALU.add
+    )
+    half_turns = pool.tile([P, 4, width], I32)
+    nc.vector.tensor_scalar(out=half_turns[:], in0=shifted[:], scalar1=ROUND_MAGIC, scalar2=None, op0=ALU.subtract)
+    rest = pool.tile([P, 4, width], F32)
+    nc.vector.scalar_tensor_tensor(
+        out=rest[:], in0=half_turns[:], scalar=-float(HALF_TURN), in1=flat, op0=ALU.mult, op1=ALU.add
+    )
+    sine = pool.tile([P, 4, width], F32)
+    nc.scalar.activation(out=sine[:], in_=rest[:], func=ACT.Sin, scale=math.pi / HALF_TURN)
+    odd = pool.tile([P, 4, width], I32)
+    nc.vector.tensor_scalar(out=odd[:], in0=half_turns[:], scalar1=1, scalar2=None, op0=ALU.bitwise_and)
+    sign = pool.tile([P, 4, width], F32)
+    nc.vector.tensor_scalar(out=sign[:], in0=odd[:], scalar1=-2.0, scalar2=1.0, op0=ALU.mult, op1=ALU.add)
+
+    tables = pool.tile([P, 2, GROUPS, ROTATED], F32)
+    for c in range(2):
+        pairs = tables[:, c].rearrange("p j (i e) -> p j i e", e=2)
+        factors = [values[:, 2 * c : 2 * c + 2, :].rearrange("p e w -> p w e") for values in (sine, sign)]
+        shape = [P, GROUPS, SHARED_PAIRS, 2]
         nc.vector.tensor_tensor(
-            out=sines[:].rearrange("p j (i e) -> p (j i) e", e=2)[:, :, e],
-            in0=sine[:, phase, :],
-            in1=sign[:, phase, :],
+            out=pairs[:, :, :SHARED_PAIRS, :],
+            in0=factors[0][:, :SHARED_PAIRS, :].unsqueeze(1).to_broadcast(shape),
+            in1=factors[1][:, :SHARED_PAIRS, :].unsqueeze(1).to_broadcast(shape),
             op=ALU.mult,
         )
-    return cosines, sines
+        nc.vector.tensor_tensor(
+            out=pairs[:, :, SHARED_PAIRS:, :],
+            in0=factors[0][:, SHARED_PAIRS:, :].rearrange("p (j f) e -> p j f e", f=FREQS),
+            in1=factors[1][:, SHARED_PAIRS:, :].rearrange("p (j f) e -> p j f e", f=FREQS),
+            op=ALU.mult,
+        )
+    return tables
 
 
 def tile_attention_pa_kernel(tc, x, Wqkv_words, Wqkv_scales, out_0, out_1, out_2):
@@ -129,131 +154,174 @@ def tile_attention_pa_kernel(tc, x, Wqkv_words, Wqkv_scales, out_0, out_1, out_2
     outs = (out_0, out_1, out_2)
     with ExitStack() as ctx:
         keep = ctx.enter_context(tc.tile_pool(name="keep", bufs=1))
-        regroup = ctx.enter_context(tc.tile_pool(name="regroup", bufs=GROUPS))
-        results = ctx.enter_context(tc.tile_pool(name="results", bufs=6))
+        regroup = ctx.enter_context(tc.tile_pool(name="regroup", bufs=4))
+        rotated_results = ctx.enter_context(tc.tile_pool(name="rotated_results", bufs=6))
+        plain_results = ctx.enter_context(tc.tile_pool(name="plain_results", bufs=2))
         crosses = ctx.enter_context(tc.tile_pool(name="crosses", bufs=4))
         psum = ctx.enter_context(tc.psum_pool(name="psum", bufs=8))
 
-        x_rows = [keep.tile([P, GROUPS, CHANNELS], BF16, name="x_rows%d" % b) for b in range(BATCH)]
-        x_codes = keep.tile([P, BATCH, GROUPS, PASSES * P], U32, align_bytes=64)
-        x_scales = keep.tile([P, BATCH, GROUPS, PASSES * P], U8, align_bytes=64)
+        x_rows = {}
+        x_codes = keep.tile([P, GROUPS, PASSES * P], U32, align_bytes=64)
+        x_scales = keep.tile([P, GROUPS, PASSES * P], U8, align_bytes=64)
         w_codes = keep.tile([P, PASSES, COLUMNS], U32, align_bytes=64)
         w_scales = keep.tile([P, PASSES, COLUMNS], U8, align_bytes=64)
 
         nc.vector.memset(w_scales[:].bitcast(I32), 0)
 
-        def load_x(b):
-            nc.sync.dma_start(
-                out=x_rows[b][:].rearrange("p j k -> p (j k)"),
-                in_=x[b].rearrange("(p j) k -> p (j k)", j=GROUPS),
-            )
+        def load_x(groups):
+            count = groups.stop - groups.start
+            rows = keep.tile([P, count, CHANNELS], BF16, name="x_rows%d" % groups.start)
+            for b in range(BATCH):
+                nc.sync.dma_start(
+                    out=rows[b:P:BATCH],
+                    in_=x[b].rearrange("(r j) k -> r j k", j=GROUPS)[:, groups, :],
+                )
+            for a in range(count):
+                x_rows[groups.start + a] = rows[:, a, :]
 
-        def load_w_scales():
+        def load_w_scales(first_column, columns):
+            words = slice(first_column // 4, (first_column + columns) // 4)
             rows = Wqkv_scales.bitcast(I32).rearrange("g q n -> q g n")
             plane = w_scales[:].bitcast(I32)
             for quadrant in range(4):
                 nc.sync.dma_start(
-                    out=plane[32 * quadrant : 32 * quadrant + 4], in_=rows[4 * quadrant : 4 * quadrant + 4]
+                    out=plane[32 * quadrant : 32 * quadrant + 4, :, words],
+                    in_=rows[4 * quadrant : 4 * quadrant + 4, :, words],
                 )
 
-        def block_columns(which, half):
-            first = (which * HALVES + half) * N_TILE
-            return slice(first, first + N_TILE)
+        def head_columns(which, first_head, heads):
+            first = (which * HEADS + first_head) * HEAD_DIM
+            return slice(first, first + heads * HEAD_DIM)
 
-        def load_w_codes(which, half):
+        def load_w_codes(which, first_head, heads):
             words = Wqkv_words.rearrange("g p n t -> g p (n t)").bitcast(I32).rearrange("g p n -> p g n")
-            cols = block_columns(which, half)
+            cols = head_columns(which, first_head, heads)
             nc.sync.dma_start(out=w_codes[:, :, cols].bitcast(I32), in_=words[:, :, cols])
 
-        load_x(0)
-        load_w_scales()
-        load_w_codes(Q, 0)
-        load_x(1)
-        load_w_codes(V, 0)
-        load_w_codes(K, 0)
-        for which in (Q, V, K):
-            load_w_codes(which, 1)
+        load_x(slice(0, 2))
+        load_x(slice(2, 4))
+        load_x(slice(4, 8))
+        load_w_scales(V * HEADS * HEAD_DIM, HEADS * HEAD_DIM)
+        load_w_codes(V, 0, 8)
+        load_w_scales(0, V * HEADS * HEAD_DIM)
+        load_w_codes(Q, 0, 8)
+        load_w_codes(V, 8, 8)
+        load_w_codes(K, 0, 8)
+        load_w_codes(Q, 8, 8)
+        load_w_codes(K, 8, 8)
 
+        tables = build_rotation_tables(nc, keep)
+        cosines = tables[:, 0]
+        sines = tables[:, 1]
         identity = keep.tile([P, P], F32)
         make_identity(nc, identity[:])
-        cosines, sines = build_rotation_tables(nc, keep)
 
-        def transpose_tokens(b):
-            grouped_tiles = []
-            for j in range(GROUPS):
-                words = x_rows[b][:, j, :].bitcast(F32)
-                bank = psum.tile([P, PASSES, 2, P], F32, tag="bank", name="x_bank")
-                for g in range(PASSES):
-                    for u in range(2):
-                        pass_words = slice(g * WORDS_PER_PASS + u, (g + 1) * WORDS_PER_PASS, 2)
-                        nc.tensor.transpose(bank[:, g, u, :], words[:, pass_words], identity[:])
-                grouped = regroup.tile([P, PASSES, P, PACK], BF16, align_bytes=64, name="grouped")
+        def transpose_group(j):
+            words = x_rows[j].bitcast(F32)
+            bank = psum.tile([P, PASSES, 2, P], F32, tag="bank", name="x_bank")
+            for g in range(PASSES):
+                for u in range(2):
+                    pass_words = slice(g * WORDS_PER_PASS + u, (g + 1) * WORDS_PER_PASS, 2)
+                    nc.tensor.transpose(bank[:, g, u, :], words[:, pass_words], identity[:])
+            grouped = regroup.tile([P, PASSES, P, PACK], BF16, align_bytes=64, name="grouped")
+            if j % 2 == 0:
                 nc.scalar.copy(out=grouped[:].bitcast(F32), in_=bank[:].rearrange("p g u n -> p g n u"))
-                grouped_tiles.append(grouped)
-            return grouped_tiles
+            else:
+                nc.vector.tensor_copy(out=grouped[:].bitcast(F32), in_=bank[:].rearrange("p g u n -> p g n u"))
+            return grouped
 
-        def quantise_tokens(b, grouped_tiles):
-            for j in range(GROUPS):
-                nc.vector.quantize_mx(
-                    out=x_codes[:, b, j, :].bitcast(FP8X4),
-                    scales=x_scales[:, b, j, :],
-                    in_=grouped_tiles[j][:].rearrange("p g n t -> p (g n t)"),
-                )
-
-        def project_block(b, which, half):
-            cols = block_columns(which, half)
-            staged = results.tile([P, BLOCK_HEADS, GROUPS, HEAD_DIM], F32, name="staged")
-            for first_group in range(0, GROUPS, GROUPS_PER_ADD):
-                if which != V:
-                    cross = crosses.tile([P, BLOCK_HEADS, GROUPS_PER_ADD, ROTATED], F32, name="cross")
-                for j in range(first_group, first_group + GROUPS_PER_ADD):
-                    acc = psum.tile([P, BLOCK_HEADS, HEAD_DIM], F32, tag="bank", name="acc")
-                    for g in range(PASSES):
-                        tokens = slice(g * P, (g + 1) * P)
-                        nc.tensor.matmul_mx(
-                            out=acc[:].rearrange("p h d -> p (h d)"),
-                            lhsT=x_codes[:, b, j, tokens].bitcast(FP8X4),
-                            lhsT_scale=x_scales[:, b, j, tokens],
-                            rhs=w_codes[:, g, cols].bitcast(FP8X4),
-                            rhs_scale=w_scales[:, g, cols],
-                            start=(g == 0),
-                            stop=(g == PASSES - 1),
-                        )
-                    if which == V:
-                        nc.scalar.copy(out=staged[:, :, j, :], in_=acc[:])
-                        continue
-                    nc.scalar.copy(out=staged[:, :, j, ROTATED:], in_=acc[:, :, ROTATED:])
-                    nc.vector.tensor_tensor(
-                        out=staged[:, :, j, :ROTATED],
-                        in0=acc[:, :, :ROTATED],
-                        in1=cosines[:, j, :].unsqueeze(1).to_broadcast([P, BLOCK_HEADS, ROTATED]),
-                        op=ALU.mult,
-                    )
-                    shape = [P, BLOCK_HEADS, PAIRS, 2]
-                    nc.vector.tensor_tensor(
-                        out=cross[:, :, j - first_group, :].rearrange("p h (i e) -> p h i e", e=2),
-                        in0=acc[:, :, :ROTATED].rearrange("p h (i e) -> p h i e", e=2)[:, :, :, ::-1],
-                        in1=sines[:, j, :].rearrange("p (i e) -> p i e", e=2).unsqueeze(1).to_broadcast(shape),
-                        op=ALU.mult,
-                    )
-                if which != V:
-                    some = slice(first_group, first_group + GROUPS_PER_ADD)
-                    target = staged[:, :, some, :ROTATED]
-                    nc.gpsimd.tensor_tensor(out=target, in0=target, in1=cross[:], op=ALU.add)
-            heads = slice(half * BLOCK_HEADS, (half + 1) * BLOCK_HEADS)
-            nc.sync.dma_start(
-                out=outs[which][b, heads].rearrange("h (p j) d -> p h (j d)", j=GROUPS),
-                in_=staged[:].rearrange("p h j d -> p h (j d)"),
+        def quantise_group(j, grouped):
+            nc.vector.quantize_mx(
+                out=x_codes[:, j, :].bitcast(FP8X4),
+                scales=x_scales[:, j, :],
+                in_=grouped[:].rearrange("p g n t -> p (g n t)"),
             )
 
-        quantise_tokens(0, transpose_tokens(0))
-        project_block(0, Q, 0)
-        grouped_1 = transpose_tokens(1)
-        project_block(0, V, 0)
-        project_block(0, K, 0)
-        quantise_tokens(1, grouped_1)
-        for which in (Q, V, K):
-            project_block(1, which, 0)
-        for b in range(BATCH):
-            for which in (Q, V, K):
-                project_block(b, which, 1)
+        def fill_bank(block, first_group):
+            which, first_head, heads, banks_per_add = block["spec"]
+            groups_per_bank = BANK_HEADS // heads
+            groups_per_add = groups_per_bank * banks_per_add
+            cols = head_columns(which, first_head, heads)
+            if first_group == 0:
+                pool = plain_results if which == V else rotated_results
+                block["staged"] = pool.tile([P, heads, GROUPS, HEAD_DIM], F32, name="staged")
+            staged = block["staged"]
+            acc = psum.tile([P, groups_per_bank, heads, HEAD_DIM], F32, tag="bank", name="acc")
+            for a in range(groups_per_bank):
+                for g in range(PASSES):
+                    tokens = slice(g * P, (g + 1) * P)
+                    nc.tensor.matmul_mx(
+                        out=acc[:, a].rearrange("p h d -> p (h d)"),
+                        lhsT=x_codes[:, first_group + a, tokens].bitcast(FP8X4),
+                        lhsT_scale=x_scales[:, first_group + a, tokens],
+                        rhs=w_codes[:, g, cols].bitcast(FP8X4),
+                        rhs_scale=w_scales[:, g, cols],
+                        start=(g == 0),
+                        stop=(g == PASSES - 1),
+                    )
+            some = slice(first_group, first_group + groups_per_bank)
+            target = staged[:, :, some, :].rearrange("p h a d -> p a h d")
+            if which == V:
+                nc.scalar.copy(out=target, in_=acc[:])
+            else:
+                nc.scalar.copy(out=target[:, :, :, ROTATED:], in_=acc[:, :, :, ROTATED:])
+                nc.vector.tensor_tensor(
+                    out=target[:, :, :, :ROTATED],
+                    in0=acc[:, :, :, :ROTATED],
+                    in1=cosines[:, some, :].unsqueeze(2).to_broadcast([P, groups_per_bank, heads, ROTATED]),
+                    op=ALU.mult,
+                )
+                place = first_group % groups_per_add
+                if place == 0:
+                    block["cross"] = crosses.tile([P, groups_per_add, heads, ROTATED], F32, name="cross")
+                cross = block["cross"]
+                nc.vector.tensor_tensor(
+                    out=cross[:, place : place + groups_per_bank].rearrange("p a h (i e) -> p a h i e", e=2),
+                    in0=acc[:, :, :, :ROTATED].rearrange("p a h (i e) -> p a h i e", e=2)[:, :, :, :, ::-1],
+                    in1=sines[:, some, :]
+                    .rearrange("p a (i e) -> p a i e", e=2)
+                    .unsqueeze(2)
+                    .to_broadcast([P, groups_per_bank, heads, PAIRS, 2]),
+                    op=ALU.mult,
+                )
+                if place + groups_per_bank == groups_per_add:
+                    joined = slice(first_group + groups_per_bank - groups_per_add, first_group + groups_per_bank)
+                    nc.gpsimd.tensor_tensor(
+                        out=staged[:, :, joined, :ROTATED],
+                        in0=staged[:, :, joined, :ROTATED],
+                        in1=cross[:].rearrange("p a h d -> p h a d"),
+                        op=ALU.add,
+                    )
+            if first_group + groups_per_bank == GROUPS:
+                queue = nc.scalar if which == V else nc.sync
+                for b in range(BATCH):
+                    queue.dma_start(
+                        out=outs[which][b, first_head : first_head + heads].rearrange(
+                            "h (r j) d -> r h (j d)", j=GROUPS
+                        ),
+                        in_=staged[b:P:BATCH].rearrange("p h j d -> p h (j d)"),
+                    )
+
+        def block_steps(which, first_head, heads, banks_per_add):
+            block = {"spec": (which, first_head, heads, banks_per_add)}
+            return [partial(fill_bank, block, j) for j in range(0, GROUPS, BANK_HEADS // heads)]
+
+        rotated_steps = []
+        for spec in ROTATED_BLOCKS:
+            rotated_steps.extend(block_steps(*spec))
+        plain_steps = []
+        for spec in PLAIN_BLOCKS:
+            plain_steps.extend(block_steps(*spec))
+
+        grouped_tiles = {}
+        for j in range(GROUPS + 1):
+            if j < GROUPS:
+                grouped_tiles[j] = transpose_group(j)
+            if j > 0:
+                quantise_group(j - 1, grouped_tiles[j - 1])
+        for fill in plain_steps[:PLAIN_LEAD]:
+            fill()
+        for step, fill in enumerate(rotated_steps):
+            fill()
+            if PLAIN_LEAD + step < len(plain_steps):
+                plain_steps[PLAIN_LEAD + step]()

@@ -38,17 +38,14 @@ PLACES = 2 + GROUPS
 Q, K, V = 0, 1, 2
 
 ROTATED_BLOCKS = (
-    (Q, 0, 4, 2),
-    (Q, 4, 4, 2),
-    (K, 0, 4, 2),
-    (K, 4, 4, 2),
-    (Q, 8, 4, 2),
-    (Q, 12, 4, 2),
-    (K, 8, 4, 2),
-    (K, 12, 4, 1),
+    (Q, 0, 8, 2, False),
+    (K, 0, 8, 2, False),
+    (Q, 8, 8, 2, False),
+    (K, 8, 4, 2, False),
+    (K, 12, 4, 2, True),
 )
-PLAIN_BLOCKS = ((V, 0, 8, 1), (V, 8, 8, 1))
-PLAIN_LEAD = 4
+PLAIN_BLOCKS = ((V, 0, 8, 1, False), (V, 8, 8, 1, False))
+PLAIN_LEAD = 0
 
 FLOPS = 2 * BATCH * TOKENS * CHANNELS * COLUMNS
 
@@ -79,7 +76,7 @@ def build_rotation_tables(nc, pool):
         start[:, 0], pattern=[[0, 2], [-210 * 127, FREQS]], base=QUARTER_TURN - 210 * 7, channel_multiplier=0
     )
     nc.gpsimd.iota(
-        start[:, 1], pattern=[[-HALF_TURN, 2], [-210 * 127, FREQS]], base=HALF_TURN - 210 * 7, channel_multiplier=0
+        start[:, 1], pattern=[[HALF_TURN, 2], [-210 * 127, FREQS]], base=-210 * 7, channel_multiplier=0
     )
 
     grid = pool.tile([P, AXES], I32)
@@ -129,21 +126,22 @@ def build_rotation_tables(nc, pool):
     sign = pool.tile([P, 4, width], F32)
     nc.vector.tensor_scalar(out=sign[:], in0=odd[:], scalar1=-2.0, scalar2=1.0, op0=ALU.mult, op1=ALU.add)
 
-    tables = pool.tile([P, 2, GROUPS, ROTATED], F32)
+    tables = pool.tile([P, GROUPS // 2, 2, 2, ROTATED], F32)
     for c in range(2):
-        pairs = tables[:, c].rearrange("p j (i e) -> p j i e", e=2)
+        pairs = tables[:, :, c].rearrange("p m a (i e) -> p m a i e", e=2)
         factors = [values[:, 2 * c : 2 * c + 2, :].rearrange("p e w -> p w e") for values in (sine, sign)]
-        shape = [P, GROUPS, SHARED_PAIRS, 2]
+        shape = [P, GROUPS // 2, SHARED_PAIRS, 2]
+        for a in range(2):
+            nc.vector.tensor_tensor(
+                out=pairs[:, :, a, :SHARED_PAIRS, :],
+                in0=factors[0][:, :SHARED_PAIRS, :].unsqueeze(1).to_broadcast(shape),
+                in1=factors[1][:, :SHARED_PAIRS, :].unsqueeze(1).to_broadcast(shape),
+                op=ALU.mult,
+            )
         nc.vector.tensor_tensor(
-            out=pairs[:, :, :SHARED_PAIRS, :],
-            in0=factors[0][:, :SHARED_PAIRS, :].unsqueeze(1).to_broadcast(shape),
-            in1=factors[1][:, :SHARED_PAIRS, :].unsqueeze(1).to_broadcast(shape),
-            op=ALU.mult,
-        )
-        nc.vector.tensor_tensor(
-            out=pairs[:, :, SHARED_PAIRS:, :],
-            in0=factors[0][:, SHARED_PAIRS:, :].rearrange("p (j f) e -> p j f e", f=FREQS),
-            in1=factors[1][:, SHARED_PAIRS:, :].rearrange("p (j f) e -> p j f e", f=FREQS),
+            out=pairs[:, :, :, SHARED_PAIRS:, :],
+            in0=factors[0][:, SHARED_PAIRS:, :].rearrange("p (m a f) e -> p m a f e", a=2, f=FREQS),
+            in1=factors[1][:, SHARED_PAIRS:, :].rearrange("p (m a f) e -> p m a f e", a=2, f=FREQS),
             op=ALU.mult,
         )
     return tables
@@ -155,7 +153,7 @@ def tile_attention_pa_kernel(tc, x, Wqkv_words, Wqkv_scales, out_0, out_1, out_2
     with ExitStack() as ctx:
         keep = ctx.enter_context(tc.tile_pool(name="keep", bufs=1))
         regroup = ctx.enter_context(tc.tile_pool(name="regroup", bufs=4))
-        rotated_results = ctx.enter_context(tc.tile_pool(name="rotated_results", bufs=6))
+        rotated_results = ctx.enter_context(tc.tile_pool(name="rotated_results", bufs=4))
         plain_results = ctx.enter_context(tc.tile_pool(name="plain_results", bufs=2))
         crosses = ctx.enter_context(tc.tile_pool(name="crosses", bufs=4))
         psum = ctx.enter_context(tc.psum_pool(name="psum", bufs=8))
@@ -201,18 +199,16 @@ def tile_attention_pa_kernel(tc, x, Wqkv_words, Wqkv_scales, out_0, out_1, out_2
         load_x(slice(0, 2))
         load_x(slice(2, 4))
         load_x(slice(4, 8))
-        load_w_scales(V * HEADS * HEAD_DIM, HEADS * HEAD_DIM)
-        load_w_codes(V, 0, 8)
         load_w_scales(0, V * HEADS * HEAD_DIM)
         load_w_codes(Q, 0, 8)
+        load_w_scales(V * HEADS * HEAD_DIM, HEADS * HEAD_DIM)
+        load_w_codes(V, 0, 8)
         load_w_codes(V, 8, 8)
         load_w_codes(K, 0, 8)
         load_w_codes(Q, 8, 8)
         load_w_codes(K, 8, 8)
 
         tables = build_rotation_tables(nc, keep)
-        cosines = tables[:, 0]
-        sines = tables[:, 1]
         identity = keep.tile([P, P], F32)
         make_identity(nc, identity[:])
 
@@ -224,10 +220,7 @@ def tile_attention_pa_kernel(tc, x, Wqkv_words, Wqkv_scales, out_0, out_1, out_2
                     pass_words = slice(g * WORDS_PER_PASS + u, (g + 1) * WORDS_PER_PASS, 2)
                     nc.tensor.transpose(bank[:, g, u, :], words[:, pass_words], identity[:])
             grouped = regroup.tile([P, PASSES, P, PACK], BF16, align_bytes=64, name="grouped")
-            if j % 2 == 0:
-                nc.scalar.copy(out=grouped[:].bitcast(F32), in_=bank[:].rearrange("p g u n -> p g n u"))
-            else:
-                nc.vector.tensor_copy(out=grouped[:].bitcast(F32), in_=bank[:].rearrange("p g u n -> p g n u"))
+            nc.scalar.copy(out=grouped[:].bitcast(F32), in_=bank[:].rearrange("p g u n -> p g n u"))
             return grouped
 
         def quantise_group(j, grouped):
@@ -238,9 +231,8 @@ def tile_attention_pa_kernel(tc, x, Wqkv_words, Wqkv_scales, out_0, out_1, out_2
             )
 
         def fill_bank(block, first_group):
-            which, first_head, heads, banks_per_add = block["spec"]
+            which, first_head, heads, groups_per_add, vector_adds = block["spec"]
             groups_per_bank = BANK_HEADS // heads
-            groups_per_add = groups_per_bank * banks_per_add
             cols = head_columns(which, first_head, heads)
             if first_group == 0:
                 pool = plain_results if which == V else rotated_results
@@ -259,40 +251,35 @@ def tile_attention_pa_kernel(tc, x, Wqkv_words, Wqkv_scales, out_0, out_1, out_2
                         start=(g == 0),
                         stop=(g == PASSES - 1),
                     )
-            some = slice(first_group, first_group + groups_per_bank)
-            target = staged[:, :, some, :].rearrange("p h a d -> p a h d")
+            last_group = first_group + groups_per_bank - 1
+            target = staged[:, :, first_group : last_group + 1, :].rearrange("p h a d -> p a h d")
             if which == V:
                 nc.scalar.copy(out=target, in_=acc[:])
             else:
-                nc.scalar.copy(out=target[:, :, :, ROTATED:], in_=acc[:, :, :, ROTATED:])
-                nc.vector.tensor_tensor(
-                    out=target[:, :, :, :ROTATED],
-                    in0=acc[:, :, :, :ROTATED],
-                    in1=cosines[:, some, :].unsqueeze(2).to_broadcast([P, groups_per_bank, heads, ROTATED]),
-                    op=ALU.mult,
-                )
                 place = first_group % groups_per_add
                 if place == 0:
-                    block["cross"] = crosses.tile([P, groups_per_add, heads, ROTATED], F32, name="cross")
-                cross = block["cross"]
+                    block["products"] = crosses.tile([P, 2, groups_per_add, heads, ROTATED], F32, name="products")
+                products = block["products"]
+                shape = [P, 2, groups_per_bank, heads, ROTATED]
+                of_groups = tables[:, first_group // 2, :, first_group % 2 : first_group % 2 + groups_per_bank, :]
                 nc.vector.tensor_tensor(
-                    out=cross[:, place : place + groups_per_bank].rearrange("p a h (i e) -> p a h i e", e=2),
-                    in0=acc[:, :, :, :ROTATED].rearrange("p a h (i e) -> p a h i e", e=2)[:, :, :, :, ::-1],
-                    in1=sines[:, some, :]
-                    .rearrange("p a (i e) -> p a i e", e=2)
-                    .unsqueeze(2)
-                    .to_broadcast([P, groups_per_bank, heads, PAIRS, 2]),
+                    out=products[:, :, place : place + groups_per_bank],
+                    in0=acc[:, :, :, :ROTATED].unsqueeze(1).to_broadcast(shape),
+                    in1=of_groups.unsqueeze(3).to_broadcast(shape),
                     op=ALU.mult,
                 )
+                nc.scalar.copy(out=target[:, :, :, ROTATED:], in_=acc[:, :, :, ROTATED:])
                 if place + groups_per_bank == groups_per_add:
-                    joined = slice(first_group + groups_per_bank - groups_per_add, first_group + groups_per_bank)
-                    nc.gpsimd.tensor_tensor(
-                        out=staged[:, :, joined, :ROTATED],
-                        in0=staged[:, :, joined, :ROTATED],
-                        in1=cross[:].rearrange("p a h d -> p h a d"),
+                    adder = nc.vector if vector_adds else nc.gpsimd
+                    joined = slice(last_group + 1 - groups_per_add, last_group + 1)
+                    by_pairs = "p a h (i e) -> p a h i e"
+                    adder.tensor_tensor(
+                        out=staged[:, :, joined, :ROTATED].rearrange("p h a d -> p a h d").rearrange(by_pairs, e=2),
+                        in0=products[:, 0].rearrange(by_pairs, e=2),
+                        in1=products[:, 1].rearrange(by_pairs, e=2)[:, :, :, :, ::-1],
                         op=ALU.add,
                     )
-            if first_group + groups_per_bank == GROUPS:
+            if last_group == GROUPS - 1:
                 queue = nc.scalar if which == V else nc.sync
                 for b in range(BATCH):
                     queue.dma_start(
@@ -302,9 +289,9 @@ def tile_attention_pa_kernel(tc, x, Wqkv_words, Wqkv_scales, out_0, out_1, out_2
                         in_=staged[b:P:BATCH].rearrange("p h j d -> p h (j d)"),
                     )
 
-        def block_steps(which, first_head, heads, banks_per_add):
-            block = {"spec": (which, first_head, heads, banks_per_add)}
-            return [partial(fill_bank, block, j) for j in range(0, GROUPS, BANK_HEADS // heads)]
+        def block_steps(*spec):
+            block = {"spec": spec}
+            return [partial(fill_bank, block, j) for j in range(0, GROUPS, BANK_HEADS // spec[2])]
 
         rotated_steps = []
         for spec in ROTATED_BLOCKS:

@@ -38,13 +38,16 @@ PLACES = 2 + GROUPS
 Q, K, V = 0, 1, 2
 
 ROTATED_BLOCKS = (
-    (Q, 0, 8, 2, False),
-    (K, 0, 8, 2, False),
-    (Q, 8, 8, 2, False),
-    (K, 8, 4, 2, False),
+    (Q, 0, 4, 4, False),
+    (Q, 4, 4, 4, False),
+    (K, 0, 4, 4, False),
+    (K, 4, 4, 4, False),
+    (Q, 8, 4, 4, False),
+    (Q, 12, 4, 4, False),
+    (K, 8, 4, 4, False),
     (K, 12, 4, 2, True),
 )
-PLAIN_BLOCKS = ((V, 0, 8, 1, False), (V, 8, 8, 1, False))
+PLAIN_BLOCKS = ((V, 0, 4, 1, False), (V, 4, 4, 1, False), (V, 8, 4, 1, False), (V, 12, 4, 1, False))
 PLAIN_LEAD = 0
 
 FLOPS = 2 * BATCH * TOKENS * CHANNELS * COLUMNS
@@ -153,8 +156,8 @@ def tile_attention_pa_kernel(tc, x, Wqkv_words, Wqkv_scales, out_0, out_1, out_2
     with ExitStack() as ctx:
         keep = ctx.enter_context(tc.tile_pool(name="keep", bufs=1))
         regroup = ctx.enter_context(tc.tile_pool(name="regroup", bufs=4))
-        rotated_results = ctx.enter_context(tc.tile_pool(name="rotated_results", bufs=4))
-        plain_results = ctx.enter_context(tc.tile_pool(name="plain_results", bufs=2))
+        rotated_results = ctx.enter_context(tc.tile_pool(name="rotated_results", bufs=6))
+        plain_results = ctx.enter_context(tc.tile_pool(name="plain_results", bufs=4))
         crosses = ctx.enter_context(tc.tile_pool(name="crosses", bufs=4))
         psum = ctx.enter_context(tc.psum_pool(name="psum", bufs=8))
 
@@ -203,8 +206,8 @@ def tile_attention_pa_kernel(tc, x, Wqkv_words, Wqkv_scales, out_0, out_1, out_2
         load_w_codes(Q, 0, 8)
         load_w_scales(V * HEADS * HEAD_DIM, HEADS * HEAD_DIM)
         load_w_codes(V, 0, 8)
-        load_w_codes(V, 8, 8)
         load_w_codes(K, 0, 8)
+        load_w_codes(V, 8, 8)
         load_w_codes(Q, 8, 8)
         load_w_codes(K, 8, 8)
 

@@ -202,10 +202,16 @@ def tile_attention_pa_kernel(tc, x, Wqkv_words, Wqkv_scales, out_0, out_1, out_2
         load_x(slice(0, 2))
         load_x(slice(2, 4))
         load_x(slice(4, 8))
-        load_w_scales(0, V * HEADS * HEAD_DIM)
-        load_w_codes(Q, 0, 8)
-        load_w_scales(V * HEADS * HEAD_DIM, HEADS * HEAD_DIM)
-        load_w_codes(V, 0, 8)
+        block_columns = 4 * HEAD_DIM
+        v_column = V * HEADS * HEAD_DIM
+        load_w_scales(0, block_columns)
+        load_w_codes(Q, 0, 4)
+        load_w_scales(v_column, block_columns)
+        load_w_codes(V, 0, 4)
+        load_w_scales(block_columns, v_column - block_columns)
+        load_w_codes(Q, 4, 4)
+        load_w_scales(v_column + block_columns, COLUMNS - v_column - block_columns)
+        load_w_codes(V, 4, 4)
         load_w_codes(K, 0, 8)
         load_w_codes(V, 8, 8)
         load_w_codes(Q, 8, 8)

@@ -201,7 +201,8 @@ def tile_attention_pa_kernel(tc, x, Wqkv_words, Wqkv_scales, out_0, out_1, out_2
 
         load_x(slice(0, 2))
         load_x(slice(2, 4))
-        load_x(slice(4, 8))
+        load_x(slice(4, 6))
+        load_x(slice(6, 8))
         block_columns = 4 * HEAD_DIM
         v_column = V * HEADS * HEAD_DIM
         load_w_scales(0, block_columns)
@@ -229,7 +230,10 @@ def tile_attention_pa_kernel(tc, x, Wqkv_words, Wqkv_scales, out_0, out_1, out_2
                     pass_words = slice(g * WORDS_PER_PASS + u, (g + 1) * WORDS_PER_PASS, 2)
                     nc.tensor.transpose(bank[:, g, u, :], words[:, pass_words], identity[:])
             grouped = regroup.tile([P, PASSES, P, PACK], BF16, align_bytes=64, name="grouped")
-            nc.scalar.copy(out=grouped[:].bitcast(F32), in_=bank[:].rearrange("p g u n -> p g n u"))
+            if j % 2 == 0:
+                nc.scalar.copy(out=grouped[:].bitcast(F32), in_=bank[:].rearrange("p g u n -> p g n u"))
+            else:
+                nc.vector.tensor_copy(out=grouped[:].bitcast(F32), in_=bank[:].rearrange("p g u n -> p g n u"))
             return grouped
 
         def quantise_group(j, grouped):
@@ -288,7 +292,15 @@ def tile_attention_pa_kernel(tc, x, Wqkv_words, Wqkv_scales, out_0, out_1, out_2
                         in1=products[:, 1].rearrange(by_pairs, e=2)[:, :, :, :, ::-1],
                         op=ALU.add,
                     )
-            if last_group == GROUPS - 1:
+                    if vector_adds:
+                        for b in range(BATCH):
+                            nc.sync.dma_start(
+                                out=outs[which][b, first_head : first_head + heads].rearrange(
+                                    "h (r j) d -> r h j d", j=GROUPS
+                                )[:, :, joined, :],
+                                in_=staged[b:P:BATCH, :, joined, :],
+                            )
+            if last_group == GROUPS - 1 and not vector_adds:
                 queue = nc.scalar if which == V else nc.sync
                 for b in range(BATCH):
                     queue.dma_start(

@@ -48,7 +48,7 @@ ROTATED_BLOCKS = (
     (K, 12, 4, 2, True),
 )
 PLAIN_BLOCKS = ((V, 0, 4, 1, False), (V, 4, 4, 1, False), (V, 8, 4, 1, False), (V, 12, 4, 1, False))
-PLAIN_LEAD = 0
+PLAIN_HEAD = 4
 
 FLOPS = 2 * BATCH * TOKENS * CHANNELS * COLUMNS
 
@@ -327,9 +327,10 @@ def tile_attention_pa_kernel(tc, x, Wqkv_words, Wqkv_scales, out_0, out_1, out_2
                 grouped_tiles[j] = transpose_group(j)
             if j > 0:
                 quantise_group(j - 1, grouped_tiles[j - 1])
-        for fill in plain_steps[:PLAIN_LEAD]:
-            fill()
+        done = 0
         for step, fill in enumerate(rotated_steps):
             fill()
-            if PLAIN_LEAD + step < len(plain_steps):
-                plain_steps[PLAIN_LEAD + step]()
+            due = step + 1 if step < PLAIN_HEAD else PLAIN_HEAD + (step + 1 - PLAIN_HEAD) // 2
+            for plain in plain_steps[done:due]:
+                plain()
+            done = due

@@ -38,16 +38,18 @@ PLACES = 2 + GROUPS
 Q, K, V = 0, 1, 2
 
 ROTATED_BLOCKS = (
+    (K, 12, 4, 4, False),
     (Q, 0, 4, 4, False),
     (Q, 4, 4, 4, False),
-    (K, 0, 4, 4, False),
-    (K, 4, 4, 4, False),
     (Q, 8, 4, 4, False),
     (Q, 12, 4, 4, False),
-    (K, 8, 4, 4, False),
-    (K, 12, 4, 2, True),
+    (K, 0, 4, 4, False),
+    (K, 4, 4, 4, False),
+    (K, 8, 4, 2, True),
 )
 PLAIN_BLOCKS = ((V, 0, 4, 1, False), (V, 4, 4, 1, False), (V, 8, 4, 1, False), (V, 12, 4, 1, False))
+FIRST_COLUMN = (2 * HEADS - 4) * HEAD_DIM
+FIRST_COLUMNS = 8 * HEAD_DIM
 PLAIN_HEAD = 4
 
 FLOPS = 2 * BATCH * TOKENS * CHANNELS * COLUMNS
@@ -194,29 +196,23 @@ def tile_attention_pa_kernel(tc, x, Wqkv_words, Wqkv_scales, out_0, out_1, out_2
             first = (which * HEADS + first_head) * HEAD_DIM
             return slice(first, first + heads * HEAD_DIM)
 
-        def load_w_codes(which, first_head, heads):
+        def load_w_codes(first_column, columns):
             words = Wqkv_words.rearrange("g p n t -> g p (n t)").bitcast(I32).rearrange("g p n -> p g n")
-            cols = head_columns(which, first_head, heads)
+            cols = slice(first_column, first_column + columns)
             nc.sync.dma_start(out=w_codes[:, :, cols].bitcast(I32), in_=words[:, :, cols])
 
         load_x(slice(0, 2))
         load_x(slice(2, 4))
         load_x(slice(4, 6))
         load_x(slice(6, 8))
-        block_columns = 4 * HEAD_DIM
-        v_column = V * HEADS * HEAD_DIM
-        load_w_scales(0, block_columns)
-        load_w_codes(Q, 0, 4)
-        load_w_scales(v_column, block_columns)
-        load_w_codes(V, 0, 4)
-        load_w_scales(block_columns, v_column - block_columns)
-        load_w_codes(Q, 4, 4)
-        load_w_scales(v_column + block_columns, COLUMNS - v_column - block_columns)
-        load_w_codes(V, 4, 4)
-        load_w_codes(K, 0, 8)
-        load_w_codes(V, 8, 8)
-        load_w_codes(Q, 8, 8)
-        load_w_codes(K, 8, 8)
+        load_w_scales(FIRST_COLUMN, FIRST_COLUMNS)
+        load_w_codes(FIRST_COLUMN, FIRST_COLUMNS)
+        load_w_scales(0, FIRST_COLUMN)
+        load_w_codes(0, 8 * HEAD_DIM)
+        load_w_scales(FIRST_COLUMN + FIRST_COLUMNS, COLUMNS - FIRST_COLUMN - FIRST_COLUMNS)
+        load_w_codes(FIRST_COLUMN + FIRST_COLUMNS, COLUMNS - FIRST_COLUMN - FIRST_COLUMNS)
+        load_w_codes(8 * HEAD_DIM, 8 * HEAD_DIM)
+        load_w_codes(16 * HEAD_DIM, FIRST_COLUMN - 16 * HEAD_DIM)
 
         tables = build_rotation_tables(nc, keep)
         identity = keep.tile([P, P], F32)

@@ -174,11 +174,12 @@ def tile_attention_pa_kernel(tc, x, Wqkv_words, Wqkv_scales, out_0, out_1, out_2
         def load_x(groups):
             count = groups.stop - groups.start
             rows = keep.tile([P, count, CHANNELS], BF16, name="x_rows%d" % groups.start)
-            for b in range(BATCH):
-                nc.sync.dma_start(
-                    out=rows[b:P:BATCH],
-                    in_=x[b].rearrange("(r j) k -> r j k", j=GROUPS)[:, groups, :],
-                )
+            nc.sync.dma_start(
+                out=rows[:].rearrange("p j k -> p (j k)"),
+                in_=x.rearrange("b (r j) k -> r b (j k)", j=GROUPS)[
+                    :, :, groups.start * CHANNELS : groups.stop * CHANNELS
+                ],
+            )
             for a in range(count):
                 x_rows[groups.start + a] = rows[:, a, :]
 
@@ -239,13 +240,18 @@ def tile_attention_pa_kernel(tc, x, Wqkv_words, Wqkv_scales, out_0, out_1, out_2
                 in_=grouped[:].rearrange("p g n t -> p (g n t)"),
             )
 
+        def rows_of_head(which, head):
+            return outs[which][:, head].rearrange("b (r j) d -> r b (j d)", j=GROUPS)
+
         def fill_bank(block, first_group):
             which, first_head, heads, groups_per_add, vector_adds = block["spec"]
             groups_per_bank = BANK_HEADS // heads
             cols = head_columns(which, first_head, heads)
-            if first_group == 0:
+            groups_per_store = groups_per_add if vector_adds else GROUPS
+            row = first_group % groups_per_store
+            if row == 0:
                 pool = plain_results if which == V else rotated_results
-                block["staged"] = pool.tile([P, heads, GROUPS, HEAD_DIM], F32, name="staged")
+                block["staged"] = pool.tile([P, heads, groups_per_store, HEAD_DIM], F32, name="staged")
             staged = block["staged"]
             acc = psum.tile([P, groups_per_bank, heads, HEAD_DIM], F32, tag="bank", name="acc")
             for a in range(groups_per_bank):
@@ -261,7 +267,7 @@ def tile_attention_pa_kernel(tc, x, Wqkv_words, Wqkv_scales, out_0, out_1, out_2
                         stop=(g == PASSES - 1),
                     )
             last_group = first_group + groups_per_bank - 1
-            target = staged[:, :, first_group : last_group + 1, :].rearrange("p h a d -> p a h d")
+            target = staged[:, :, row : row + groups_per_bank, :].rearrange("p h a d -> p a h d")
             if which == V:
                 nc.scalar.copy(out=target, in_=acc[:])
             else:
@@ -280,7 +286,7 @@ def tile_attention_pa_kernel(tc, x, Wqkv_words, Wqkv_scales, out_0, out_1, out_2
                 nc.scalar.copy(out=target[:, :, :, ROTATED:], in_=acc[:, :, :, ROTATED:])
                 if place + groups_per_bank == groups_per_add:
                     adder = nc.vector if vector_adds else nc.gpsimd
-                    joined = slice(last_group + 1 - groups_per_add, last_group + 1)
+                    joined = slice(row + groups_per_bank - groups_per_add, row + groups_per_bank)
                     by_pairs = "p a h (i e) -> p a h i e"
                     adder.tensor_tensor(
                         out=staged[:, :, joined, :ROTATED].rearrange("p h a d -> p a h d").rearrange(by_pairs, e=2),
@@ -288,22 +294,12 @@ def tile_attention_pa_kernel(tc, x, Wqkv_words, Wqkv_scales, out_0, out_1, out_2
                         in1=products[:, 1].rearrange(by_pairs, e=2)[:, :, :, :, ::-1],
                         op=ALU.add,
                     )
-                    if vector_adds:
-                        for b in range(BATCH):
-                            nc.sync.dma_start(
-                                out=outs[which][b, first_head : first_head + heads].rearrange(
-                                    "h (r j) d -> r h j d", j=GROUPS
-                                )[:, :, joined, :],
-                                in_=staged[b:P:BATCH, :, joined, :],
-                            )
-            if last_group == GROUPS - 1 and not vector_adds:
-                queue = nc.scalar if which == V else nc.sync
-                for b in range(BATCH):
-                    queue.dma_start(
-                        out=outs[which][b, first_head : first_head + heads].rearrange(
-                            "h (r j) d -> r h (j d)", j=GROUPS
-                        ),
-                        in_=staged[b:P:BATCH].rearrange("p h j d -> p h (j d)"),
+            if row + groups_per_bank == groups_per_store:
+                values = slice((last_group + 1 - groups_per_store) * HEAD_DIM, (last_group + 1) * HEAD_DIM)
+                for h in range(heads):
+                    nc.sync.dma_start(
+                        out=rows_of_head(which, first_head + h)[:, :, values],
+                        in_=staged[:, h].rearrange("p j d -> p (j d)"),
                     )
 
         def block_steps(*spec):

@@ -50,6 +50,7 @@ ROTATED_BLOCKS = (
 PLAIN_BLOCKS = ((V, 0, 4, 1, False), (V, 4, 4, 1, False), (V, 8, 4, 1, False), (V, 12, 4, 1, False))
 FIRST_COLUMN = (2 * HEADS - 4) * HEAD_DIM
 FIRST_COLUMNS = 8 * HEAD_DIM
+STORE_LAG = 2
 PLAIN_HEAD = 4
 
 FLOPS = 2 * BATCH * TOKENS * CHANNELS * COLUMNS
@@ -169,7 +170,7 @@ def tile_attention_pa_kernel(tc, x, Wqkv_words, Wqkv_scales, out_0, out_1, out_2
         w_codes = keep.tile([P, PASSES, COLUMNS], U32, align_bytes=64)
         w_scales = keep.tile([P, PASSES, COLUMNS], U8, align_bytes=64)
 
-        nc.vector.memset(w_scales[:].bitcast(I32), 0)
+        nc.gpsimd.memset(w_scales[:].bitcast(F32), 0.0)
 
         def load_x(groups):
             count = groups.stop - groups.start
@@ -227,10 +228,7 @@ def tile_attention_pa_kernel(tc, x, Wqkv_words, Wqkv_scales, out_0, out_1, out_2
                     pass_words = slice(g * WORDS_PER_PASS + u, (g + 1) * WORDS_PER_PASS, 2)
                     nc.tensor.transpose(bank[:, g, u, :], words[:, pass_words], identity[:])
             grouped = regroup.tile([P, PASSES, P, PACK], BF16, align_bytes=64, name="grouped")
-            if j % 2 == 0:
-                nc.scalar.copy(out=grouped[:].bitcast(F32), in_=bank[:].rearrange("p g u n -> p g n u"))
-            else:
-                nc.vector.tensor_copy(out=grouped[:].bitcast(F32), in_=bank[:].rearrange("p g u n -> p g n u"))
+            nc.scalar.copy(out=grouped[:].bitcast(F32), in_=bank[:].rearrange("p g u n -> p g n u"))
             return grouped
 
         def quantise_group(j, grouped):
@@ -240,10 +238,7 @@ def tile_attention_pa_kernel(tc, x, Wqkv_words, Wqkv_scales, out_0, out_1, out_2
                 in_=grouped[:].rearrange("p g n t -> p (g n t)"),
             )
 
-        def rows_of_head(which, head):
-            return outs[which][:, head].rearrange("b (r j) d -> r b (j d)", j=GROUPS)
-
-        def fill_bank(block, first_group):
+        def fill_bank(block, first_group, step):
             which, first_head, heads, groups_per_add, vector_adds = block["spec"]
             groups_per_bank = BANK_HEADS // heads
             cols = head_columns(which, first_head, heads)
@@ -296,16 +291,33 @@ def tile_attention_pa_kernel(tc, x, Wqkv_words, Wqkv_scales, out_0, out_1, out_2
                     )
             if row + groups_per_bank == groups_per_store:
                 values = slice((last_group + 1 - groups_per_store) * HEAD_DIM, (last_group + 1) * HEAD_DIM)
+                store = partial(store_block, which, first_head, heads, values, staged)
+                if which == V or vector_adds:
+                    store()
+                else:
+                    waiting_stores.extend([(step + STORE_LAG, store)])
+
+        def store_block(which, first_head, heads, values, staged):
+            if values.stop - values.start == GROUPS * HEAD_DIM:
                 for h in range(heads):
                     nc.sync.dma_start(
-                        out=rows_of_head(which, first_head + h)[:, :, values],
+                        out=outs[which][:, first_head + h].rearrange("b (r j) d -> r b (j d)", j=GROUPS),
                         in_=staged[:, h].rearrange("p j d -> p (j d)"),
+                    )
+            else:
+                for b in range(BATCH):
+                    nc.sync.dma_start(
+                        out=outs[which][b, first_head : first_head + heads].rearrange(
+                            "h (r j) d -> r h (j d)", j=GROUPS
+                        )[:, :, values],
+                        in_=staged[b:P:BATCH].rearrange("p h j d -> p h (j d)"),
                     )
 
         def block_steps(*spec):
             block = {"spec": spec}
             return [partial(fill_bank, block, j) for j in range(0, GROUPS, BANK_HEADS // spec[2])]
 
+        waiting_stores = []
         rotated_steps = []
         for spec in ROTATED_BLOCKS:
             rotated_steps.extend(block_steps(*spec))
@@ -321,8 +333,10 @@ def tile_attention_pa_kernel(tc, x, Wqkv_words, Wqkv_scales, out_0, out_1, out_2
                 quantise_group(j - 1, grouped_tiles[j - 1])
         done = 0
         for step, fill in enumerate(rotated_steps):
-            fill()
+            fill(step)
             due = step + 1 if step < PLAIN_HEAD else PLAIN_HEAD + (step + 1 - PLAIN_HEAD) // 2
             for plain in plain_steps[done:due]:
-                plain()
+                plain(step)
             done = due
+            for store in [s for when, s in waiting_stores if when == step]:
+                store()

@@ -48,6 +48,8 @@ ROTATED_BLOCKS = (
     (K, 8, 4, 2, True),
 )
 PLAIN_BLOCKS = ((V, 0, 4, 1, False), (V, 4, 4, 1, False), (V, 8, 4, 1, False), (V, 12, 4, 1, False))
+PLANES = 4
+PLANE_COLUMNS = COLUMNS // PLANES
 FIRST_COLUMN = (2 * HEADS - 4) * HEAD_DIM
 FIRST_COLUMNS = 8 * HEAD_DIM
 STORE_LAG = 2
@@ -168,9 +170,11 @@ def tile_attention_pa_kernel(tc, x, Wqkv_words, Wqkv_scales, out_0, out_1, out_2
         x_codes = keep.tile([P, GROUPS, PASSES * P], U32, align_bytes=64)
         x_scales = keep.tile([P, GROUPS, PASSES * P], U8, align_bytes=64)
         w_codes = keep.tile([P, PASSES, COLUMNS], U32, align_bytes=64)
-        w_scales = keep.tile([P, PASSES, COLUMNS], U8, align_bytes=64)
+        w_scales = keep.tile([P, PASSES, PLANE_COLUMNS], U8, align_bytes=64)
+        first_scales = keep.tile([P, PASSES, FIRST_COLUMNS], U8, align_bytes=64)
 
-        nc.gpsimd.memset(w_scales[:].bitcast(F32), 0.0)
+        nc.vector.memset(first_scales[:].bitcast(I32), 0)
+        nc.vector.memset(w_scales[:].bitcast(I32), 0)
 
         def load_x(groups):
             count = groups.stop - groups.start
@@ -184,15 +188,32 @@ def tile_attention_pa_kernel(tc, x, Wqkv_words, Wqkv_scales, out_0, out_1, out_2
             for a in range(count):
                 x_rows[groups.start + a] = rows[:, a, :]
 
-        def load_w_scales(first_column, columns):
-            words = slice(first_column // 4, (first_column + columns) // 4)
+        def load_w_scales():
+            rows = Wqkv_scales.bitcast(I32).rearrange("g q (c n) -> g c q n", c=PLANES)
+            planes = w_scales[:].bitcast(I32)
+            for g in range(PASSES):
+                for quadrant in range(4):
+                    nc.sync.dma_start(
+                        out=planes[32 * quadrant : 32 * quadrant + 4 * PLANES, g, :],
+                        in_=rows[g, :, 4 * quadrant : 4 * quadrant + 4, :],
+                    )
+
+        def load_first_scales():
+            words = slice(FIRST_COLUMN // 4, (FIRST_COLUMN + FIRST_COLUMNS) // 4)
             rows = Wqkv_scales.bitcast(I32).rearrange("g q n -> q g n")
-            plane = w_scales[:].bitcast(I32)
+            planes = first_scales[:].bitcast(I32)
             for quadrant in range(4):
                 nc.sync.dma_start(
-                    out=plane[32 * quadrant : 32 * quadrant + 4, :, words],
+                    out=planes[32 * quadrant : 32 * quadrant + 4, :, :],
                     in_=rows[4 * quadrant : 4 * quadrant + 4, :, words],
                 )
+
+        def scale_plane(g, cols):
+            if cols.start >= FIRST_COLUMN and cols.stop <= FIRST_COLUMN + FIRST_COLUMNS:
+                return first_scales[:, g, cols.start - FIRST_COLUMN : cols.stop - FIRST_COLUMN]
+            quarter = cols.start // PLANE_COLUMNS
+            first = cols.start % PLANE_COLUMNS
+            return w_scales[4 * quarter : P, g, first : first + cols.stop - cols.start]
 
         def head_columns(which, first_head, heads):
             first = (which * HEADS + first_head) * HEAD_DIM
@@ -207,13 +228,11 @@ def tile_attention_pa_kernel(tc, x, Wqkv_words, Wqkv_scales, out_0, out_1, out_2
         load_x(slice(2, 4))
         load_x(slice(4, 6))
         load_x(slice(6, 8))
-        load_w_scales(FIRST_COLUMN, FIRST_COLUMNS)
+        load_first_scales()
         load_w_codes(FIRST_COLUMN, FIRST_COLUMNS)
-        load_w_scales(0, FIRST_COLUMN)
-        load_w_codes(0, 8 * HEAD_DIM)
-        load_w_scales(FIRST_COLUMN + FIRST_COLUMNS, COLUMNS - FIRST_COLUMN - FIRST_COLUMNS)
+        load_w_scales()
+        load_w_codes(0, 16 * HEAD_DIM)
         load_w_codes(FIRST_COLUMN + FIRST_COLUMNS, COLUMNS - FIRST_COLUMN - FIRST_COLUMNS)
-        load_w_codes(8 * HEAD_DIM, 8 * HEAD_DIM)
         load_w_codes(16 * HEAD_DIM, FIRST_COLUMN - 16 * HEAD_DIM)
 
         tables = build_rotation_tables(nc, keep)
@@ -257,7 +276,7 @@ def tile_attention_pa_kernel(tc, x, Wqkv_words, Wqkv_scales, out_0, out_1, out_2
                         lhsT=x_codes[:, first_group + a, tokens].bitcast(FP8X4),
                         lhsT_scale=x_scales[:, first_group + a, tokens],
                         rhs=w_codes[:, g, cols].bitcast(FP8X4),
-                        rhs_scale=w_scales[:, g, cols],
+                        rhs_scale=scale_plane(g, cols),
                         start=(g == 0),
                         stop=(g == PASSES - 1),
                     )
@@ -333,10 +352,10 @@ def tile_attention_pa_kernel(tc, x, Wqkv_words, Wqkv_scales, out_0, out_1, out_2
                 quantise_group(j - 1, grouped_tiles[j - 1])
         done = 0
         for step, fill in enumerate(rotated_steps):
-            fill(step)
             due = step + 1 if step < PLAIN_HEAD else PLAIN_HEAD + (step + 1 - PLAIN_HEAD) // 2
             for plain in plain_steps[done:due]:
                 plain(step)
             done = due
+            fill(step)
             for store in [s for when, s in waiting_stores if when == step]:
                 store()

@@ -25,6 +25,7 @@ PACK = 4
 K_PASS = P * PACK
 PASSES = CHANNELS // K_PASS
 WORDS_PER_PASS = K_PASS // 2
+BANK_WORDS = 512
 BANK_HEADS = 8
 COLUMNS = 3 * HEADS * HEAD_DIM
 
@@ -47,7 +48,13 @@ ROTATED_BLOCKS = (
     (K, 4, 4, 4, False),
     (K, 8, 4, 2, True),
 )
-PLAIN_BLOCKS = ((V, 0, 4, 1, False), (V, 4, 4, 1, False), (V, 8, 4, 1, False), (V, 12, 4, 1, False))
+PLAIN_BLOCKS = (
+    (V, 0, 2, 1, False),
+    (V, 2, 2, 1, False),
+    (V, 4, 4, 1, False),
+    (V, 8, 4, 1, False),
+    (V, 12, 4, 1, False),
+)
 PLANES = 4
 PLANE_COLUMNS = COLUMNS // PLANES
 FIRST_COLUMN = (2 * HEADS - 4) * HEAD_DIM
@@ -163,7 +170,7 @@ def tile_attention_pa_kernel(tc, x, Wqkv_words, Wqkv_scales, out_0, out_1, out_2
         regroup = ctx.enter_context(tc.tile_pool(name="regroup", bufs=4))
         rotated_results = ctx.enter_context(tc.tile_pool(name="rotated_results", bufs=6))
         plain_results = ctx.enter_context(tc.tile_pool(name="plain_results", bufs=4))
-        crosses = ctx.enter_context(tc.tile_pool(name="crosses", bufs=4))
+        crosses = ctx.enter_context(tc.tile_pool(name="crosses", bufs=6))
         psum = ctx.enter_context(tc.psum_pool(name="psum", bufs=8))
 
         x_rows = {}
@@ -173,6 +180,8 @@ def tile_attention_pa_kernel(tc, x, Wqkv_words, Wqkv_scales, out_0, out_1, out_2
         w_scales = keep.tile([P, PASSES, PLANE_COLUMNS], U8, align_bytes=64)
         first_scales = keep.tile([P, PASSES, FIRST_COLUMNS], U8, align_bytes=64)
 
+        zeros = keep.tile([P, BANK_WORDS], BF16)
+        nc.vector.memset(zeros[:], 0.0)
         nc.vector.memset(first_scales[:].bitcast(I32), 0)
         nc.vector.memset(w_scales[:].bitcast(I32), 0)
 
@@ -249,6 +258,11 @@ def tile_attention_pa_kernel(tc, x, Wqkv_words, Wqkv_scales, out_0, out_1, out_2
             grouped = regroup.tile([P, PASSES, P, PACK], BF16, align_bytes=64, name="grouped")
             nc.scalar.copy(out=grouped[:].bitcast(F32), in_=bank[:].rearrange("p g u n -> p g n u"))
             return grouped
+
+        def warm_up(moving, count):
+            bank = psum.tile([P, BANK_WORDS], F32, tag="bank", name="warm_bank")
+            for i in range(count):
+                nc.tensor.matmul(bank[:], lhsT=zeros[:, :P], rhs=moving, start=True, stop=True)
 
         def quantise_group(j, grouped):
             nc.vector.quantize_mx(
@@ -344,18 +358,21 @@ def tile_attention_pa_kernel(tc, x, Wqkv_words, Wqkv_scales, out_0, out_1, out_2
         for spec in PLAIN_BLOCKS:
             plain_steps.extend(block_steps(*spec))
 
+        warm_up(zeros[:], 5)
         grouped_tiles = {}
         for j in range(GROUPS + 1):
+            if j == GROUPS // 2:
+                warm_up(x_rows[j][:, :BANK_WORDS], 3)
             if j < GROUPS:
                 grouped_tiles[j] = transpose_group(j)
             if j > 0:
                 quantise_group(j - 1, grouped_tiles[j - 1])
         done = 0
         for step, fill in enumerate(rotated_steps):
+            fill(step)
             due = step + 1 if step < PLAIN_HEAD else PLAIN_HEAD + (step + 1 - PLAIN_HEAD) // 2
             for plain in plain_steps[done:due]:
                 plain(step)
             done = due
-            fill(step)
             for store in [s for when, s in waiting_stores if when == step]:
                 store()

@@ -55,8 +55,6 @@ PLAIN_BLOCKS = (
     (V, 8, 4, 1, False),
     (V, 12, 4, 1, False),
 )
-PLANES = 4
-PLANE_COLUMNS = COLUMNS // PLANES
 FIRST_COLUMN = (2 * HEADS - 4) * HEAD_DIM
 FIRST_COLUMNS = 8 * HEAD_DIM
 STORE_LAG = 2
@@ -177,13 +175,15 @@ def tile_attention_pa_kernel(tc, x, Wqkv_words, Wqkv_scales, out_0, out_1, out_2
         x_codes = keep.tile([P, GROUPS, PASSES * P], U32, align_bytes=64)
         x_scales = keep.tile([P, GROUPS, PASSES * P], U8, align_bytes=64)
         w_codes = keep.tile([P, PASSES, COLUMNS], U32, align_bytes=64)
-        w_scales = keep.tile([P, PASSES, PLANE_COLUMNS], U8, align_bytes=64)
+        w_scales = keep.tile([P, PASSES, COLUMNS], U8, align_bytes=64)
         first_scales = keep.tile([P, PASSES, FIRST_COLUMNS], U8, align_bytes=64)
 
         zeros = keep.tile([P, BANK_WORDS], BF16)
         nc.vector.memset(zeros[:], 0.0)
         nc.vector.memset(first_scales[:].bitcast(I32), 0)
-        nc.vector.memset(w_scales[:].bitcast(I32), 0)
+
+        identity = keep.tile([P, P], F32)
+        make_identity(nc, identity[:])
 
         def load_x(groups):
             count = groups.stop - groups.start
@@ -197,32 +197,16 @@ def tile_attention_pa_kernel(tc, x, Wqkv_words, Wqkv_scales, out_0, out_1, out_2
             for a in range(count):
                 x_rows[groups.start + a] = rows[:, a, :]
 
-        def load_w_scales():
-            rows = Wqkv_scales.bitcast(I32).rearrange("g q (c n) -> g c q n", c=PLANES)
-            planes = w_scales[:].bitcast(I32)
-            for g in range(PASSES):
-                for quadrant in range(4):
-                    nc.sync.dma_start(
-                        out=planes[32 * quadrant : 32 * quadrant + 4 * PLANES, g, :],
-                        in_=rows[g, :, 4 * quadrant : 4 * quadrant + 4, :],
-                    )
-
-        def load_first_scales():
-            words = slice(FIRST_COLUMN // 4, (FIRST_COLUMN + FIRST_COLUMNS) // 4)
+        def load_scales(planes, first_column, columns):
+            words = slice(first_column // 4, (first_column + columns) // 4)
             rows = Wqkv_scales.bitcast(I32).rearrange("g q n -> q g n")
-            planes = first_scales[:].bitcast(I32)
-            for quadrant in range(4):
-                nc.sync.dma_start(
-                    out=planes[32 * quadrant : 32 * quadrant + 4, :, :],
-                    in_=rows[4 * quadrant : 4 * quadrant + 4, :, words],
-                )
+            for r in range(4):
+                nc.sync.dma_start(out=planes[:].bitcast(I32)[r:P:32, :, :], in_=rows[r:16:4, :, words])
 
         def scale_plane(g, cols):
             if cols.start >= FIRST_COLUMN and cols.stop <= FIRST_COLUMN + FIRST_COLUMNS:
                 return first_scales[:, g, cols.start - FIRST_COLUMN : cols.stop - FIRST_COLUMN]
-            quarter = cols.start // PLANE_COLUMNS
-            first = cols.start % PLANE_COLUMNS
-            return w_scales[4 * quarter : P, g, first : first + cols.stop - cols.start]
+            return w_scales[:, g, cols]
 
         def head_columns(which, first_head, heads):
             first = (which * HEADS + first_head) * HEAD_DIM
@@ -237,16 +221,16 @@ def tile_attention_pa_kernel(tc, x, Wqkv_words, Wqkv_scales, out_0, out_1, out_2
         load_x(slice(2, 4))
         load_x(slice(4, 6))
         load_x(slice(6, 8))
-        load_first_scales()
-        load_w_codes(FIRST_COLUMN, FIRST_COLUMNS)
-        load_w_scales()
-        load_w_codes(0, 16 * HEAD_DIM)
-        load_w_codes(FIRST_COLUMN + FIRST_COLUMNS, COLUMNS - FIRST_COLUMN - FIRST_COLUMNS)
-        load_w_codes(16 * HEAD_DIM, FIRST_COLUMN - 16 * HEAD_DIM)
-
         tables = build_rotation_tables(nc, keep)
-        identity = keep.tile([P, P], F32)
-        make_identity(nc, identity[:])
+
+        nc.gpsimd.memset(w_scales[:].bitcast(F32), 0.0)
+        load_scales(first_scales, FIRST_COLUMN, FIRST_COLUMNS)
+        load_w_codes(FIRST_COLUMN, FIRST_COLUMNS)
+        load_w_codes(0, 8 * HEAD_DIM)
+        load_scales(w_scales, 0, COLUMNS)
+        load_w_codes(FIRST_COLUMN + FIRST_COLUMNS, COLUMNS - FIRST_COLUMN - FIRST_COLUMNS)
+        load_w_codes(8 * HEAD_DIM, 8 * HEAD_DIM)
+        load_w_codes(16 * HEAD_DIM, FIRST_COLUMN - 16 * HEAD_DIM)
 
         def transpose_group(j):
             words = x_rows[j].bitcast(F32)
@@ -358,7 +342,7 @@ def tile_attention_pa_kernel(tc, x, Wqkv_words, Wqkv_scales, out_0, out_1, out_2
         for spec in PLAIN_BLOCKS:
             plain_steps.extend(block_steps(*spec))
 
-        warm_up(zeros[:], 5)
+        warm_up(zeros[:], 4)
         grouped_tiles = {}
         for j in range(GROUPS + 1):
             if j == GROUPS // 2:

@@ -57,7 +57,6 @@ PLAIN_BLOCKS = (
 )
 FIRST_COLUMN = (2 * HEADS - 4) * HEAD_DIM
 FIRST_COLUMNS = 8 * HEAD_DIM
-STORE_LAG = 2
 PLAIN_HEAD = 4
 
 FLOPS = 2 * BATCH * TOKENS * CHANNELS * COLUMNS
@@ -229,8 +228,7 @@ def tile_attention_pa_kernel(tc, x, Wqkv_words, Wqkv_scales, out_0, out_1, out_2
         load_w_codes(0, 8 * HEAD_DIM)
         load_scales(w_scales, 0, COLUMNS)
         load_w_codes(FIRST_COLUMN + FIRST_COLUMNS, COLUMNS - FIRST_COLUMN - FIRST_COLUMNS)
-        load_w_codes(8 * HEAD_DIM, 8 * HEAD_DIM)
-        load_w_codes(16 * HEAD_DIM, FIRST_COLUMN - 16 * HEAD_DIM)
+        load_w_codes(8 * HEAD_DIM, FIRST_COLUMN - 8 * HEAD_DIM)
 
         def transpose_group(j):
             words = x_rows[j].bitcast(F32)
@@ -255,15 +253,13 @@ def tile_attention_pa_kernel(tc, x, Wqkv_words, Wqkv_scales, out_0, out_1, out_2
                 in_=grouped[:].rearrange("p g n t -> p (g n t)"),
             )
 
-        def fill_bank(block, first_group, step):
+        def fill_bank(block, first_group):
             which, first_head, heads, groups_per_add, vector_adds = block["spec"]
             groups_per_bank = BANK_HEADS // heads
             cols = head_columns(which, first_head, heads)
-            groups_per_store = groups_per_add if vector_adds else GROUPS
-            row = first_group % groups_per_store
-            if row == 0:
+            if first_group == 0:
                 pool = plain_results if which == V else rotated_results
-                block["staged"] = pool.tile([P, heads, groups_per_store, HEAD_DIM], F32, name="staged")
+                block["staged"] = pool.tile([P, heads, GROUPS, HEAD_DIM], F32, name="staged")
             staged = block["staged"]
             acc = psum.tile([P, groups_per_bank, heads, HEAD_DIM], F32, tag="bank", name="acc")
             for a in range(groups_per_bank):
@@ -278,11 +274,7 @@ def tile_attention_pa_kernel(tc, x, Wqkv_words, Wqkv_scales, out_0, out_1, out_2
                         start=(g == 0),
                         stop=(g == PASSES - 1),
                     )
-            last_group = first_group + groups_per_bank - 1
-            target = staged[:, :, row : row + groups_per_bank, :].rearrange("p h a d -> p a h d")
-            if which == V:
-                nc.scalar.copy(out=target, in_=acc[:])
-            else:
+            if which != V:
                 place = first_group % groups_per_add
                 if place == 0:
                     block["products"] = crosses.tile([P, 2, groups_per_add, heads, ROTATED], F32, name="products")
@@ -295,10 +287,22 @@ def tile_attention_pa_kernel(tc, x, Wqkv_words, Wqkv_scales, out_0, out_1, out_2
                     in1=of_groups.unsqueeze(3).to_broadcast(shape),
                     op=ALU.mult,
                 )
+            return partial(empty_bank, block, first_group, acc)
+
+        def empty_bank(block, first_group, acc):
+            which, first_head, heads, groups_per_add, vector_adds = block["spec"]
+            groups_per_bank = BANK_HEADS // heads
+            last_group = first_group + groups_per_bank - 1
+            staged = block["staged"]
+            target = staged[:, :, first_group : last_group + 1, :].rearrange("p h a d -> p a h d")
+            if which == V:
+                nc.scalar.copy(out=target, in_=acc[:])
+            else:
                 nc.scalar.copy(out=target[:, :, :, ROTATED:], in_=acc[:, :, :, ROTATED:])
-                if place + groups_per_bank == groups_per_add:
+                if (last_group + 1) % groups_per_add == 0:
                     adder = nc.vector if vector_adds else nc.gpsimd
-                    joined = slice(row + groups_per_bank - groups_per_add, row + groups_per_bank)
+                    joined = slice(last_group + 1 - groups_per_add, last_group + 1)
+                    products = block["products"]
                     by_pairs = "p a h (i e) -> p a h i e"
                     adder.tensor_tensor(
                         out=staged[:, :, joined, :ROTATED].rearrange("p h a d -> p a h d").rearrange(by_pairs, e=2),
@@ -306,27 +310,13 @@ def tile_attention_pa_kernel(tc, x, Wqkv_words, Wqkv_scales, out_0, out_1, out_2
                         in1=products[:, 1].rearrange(by_pairs, e=2)[:, :, :, :, ::-1],
                         op=ALU.add,
                     )
-            if row + groups_per_bank == groups_per_store:
-                values = slice((last_group + 1 - groups_per_store) * HEAD_DIM, (last_group + 1) * HEAD_DIM)
-                store = partial(store_block, which, first_head, heads, values, staged)
-                if which == V or vector_adds:
-                    store()
-                else:
-                    waiting_stores.extend([(step + STORE_LAG, store)])
-
-        def store_block(which, first_head, heads, values, staged):
-            if values.stop - values.start == GROUPS * HEAD_DIM:
-                for h in range(heads):
-                    nc.sync.dma_start(
-                        out=outs[which][:, first_head + h].rearrange("b (r j) d -> r b (j d)", j=GROUPS),
-                        in_=staged[:, h].rearrange("p j d -> p (j d)"),
-                    )
-            else:
+            if last_group == GROUPS - 1:
+                queue = nc.scalar if which == V else nc.sync
                 for b in range(BATCH):
-                    nc.sync.dma_start(
+                    queue.dma_start(
                         out=outs[which][b, first_head : first_head + heads].rearrange(
                             "h (r j) d -> r h (j d)", j=GROUPS
-                        )[:, :, values],
+                        ),
                         in_=staged[b:P:BATCH].rearrange("p h j d -> p h (j d)"),
                     )
 
@@ -334,7 +324,6 @@ def tile_attention_pa_kernel(tc, x, Wqkv_words, Wqkv_scales, out_0, out_1, out_2
             block = {"spec": spec}
             return [partial(fill_bank, block, j) for j in range(0, GROUPS, BANK_HEADS // spec[2])]
 
-        waiting_stores = []
         rotated_steps = []
         for spec in ROTATED_BLOCKS:
             rotated_steps.extend(block_steps(*spec))
@@ -353,10 +342,9 @@ def tile_attention_pa_kernel(tc, x, Wqkv_words, Wqkv_scales, out_0, out_1, out_2
                 quantise_group(j - 1, grouped_tiles[j - 1])
         done = 0
         for step, fill in enumerate(rotated_steps):
-            fill(step)
+            empty_rotated = fill()
             due = step + 1 if step < PLAIN_HEAD else PLAIN_HEAD + (step + 1 - PLAIN_HEAD) // 2
             for plain in plain_steps[done:due]:
-                plain(step)
+                plain()()
             done = due
-            for store in [s for when, s in waiting_stores if when == step]:
-                store()
+            empty_rotated()

import math
from contextlib import ExitStack
from functools import partial

import concourse.mybir as mybir
from concourse.masks import make_identity

F32 = mybir.dt.float32
BF16 = mybir.dt.bfloat16
I32 = mybir.dt.int32
U32 = mybir.dt.uint32
U8 = mybir.dt.uint8
FP8X4 = mybir.dt.float8_e4m3fn_x4
ALU = mybir.AluOpType
ACT = mybir.ActivationFunctionType

P = 128
BATCH = 2
TOKENS = 512
CHANNELS = 1024
HEADS = 16
HEAD_DIM = 64
GROUPS = BATCH * TOKENS // P
PACK = 4
K_PASS = P * PACK
PASSES = CHANNELS // K_PASS
WORDS_PER_PASS = K_PASS // 2
BANK_WORDS = 512
BANK_HEADS = 8
COLUMNS = 3 * HEADS * HEAD_DIM

AXES = 3
FREQS = 8
PAIRS = AXES * FREQS
ROTATED = 2 * PAIRS
SHARED_PAIRS = 2 * FREQS
PLACES = 2 + GROUPS

Q, K, V = 0, 1, 2

ROTATED_BLOCKS = (
    (K, 12, 4, 4, False),
    (Q, 0, 4, 4, False),
    (Q, 4, 4, 4, False),
    (Q, 8, 4, 4, False),
    (Q, 12, 4, 4, False),
    (K, 0, 4, 4, False),
    (K, 4, 4, 4, False),
    (K, 8, 4, 2, True),
)
PLAIN_BLOCKS = (
    (V, 0, 2, 1, False),
    (V, 2, 2, 1, False),
    (V, 4, 4, 1, False),
    (V, 8, 4, 1, False),
    (V, 12, 4, 1, False),
)
FIRST_COLUMN = (2 * HEADS - 4) * HEAD_DIM
FIRST_COLUMNS = 8 * HEAD_DIM
PLAIN_HEAD = 4

FLOPS = 2 * BATCH * TOKENS * CHANNELS * COLUMNS

HALF_TURN = 2 * 105 * 7
QUARTER_TURN = HALF_TURN // 2
ROUND_MAGIC = 1.5 * 2.0**23


def build_rotation_tables(nc, pool):
    warm = pool.tile([P, 1], F32)
    nc.gpsimd.memset(warm[:], 0.0)
    nc.scalar.activation(out=warm[:], in_=warm[:], func=ACT.Sin)

    partition = pool.tile([P, 1], I32)
    nc.gpsimd.iota(partition[:], pattern=[[0, 1]], base=0, channel_multiplier=1)
    group = pool.tile([P, GROUPS], I32)
    nc.gpsimd.iota(group[:], pattern=[[1, GROUPS]], base=0, channel_multiplier=0)
    slope = pool.tile([P, PLACES, FREQS], I32)
    for step, places in ((70, slice(0, 1)), (30, slice(1, 2)), (14, slice(2, PLACES))):
        nc.gpsimd.iota(
            slope[:, places, :],
            pattern=[[0, places.stop - places.start], [2 * step * 127, FREQS]],
            base=2 * step * 7,
            channel_multiplier=0,
        )
    start = pool.tile([P, 2, 2, FREQS], I32)
    nc.gpsimd.iota(
        start[:, 0], pattern=[[0, 2], [-210 * 127, FREQS]], base=QUARTER_TURN - 210 * 7, channel_multiplier=0
    )
    nc.gpsimd.iota(
        start[:, 1], pattern=[[HALF_TURN, 2], [-210 * 127, FREQS]], base=-210 * 7, channel_multiplier=0
    )

    grid = pool.tile([P, AXES], I32)
    nc.vector.tensor_scalar(out=grid[:, 0:1], in0=partition[:], scalar1=5, scalar2=None, op0=ALU.arith_shift_right)
    nc.vector.tensor_scalar(
        out=grid[:, 1:2], in0=partition[:], scalar1=2, scalar2=7, op0=ALU.arith_shift_right, op1=ALU.bitwise_and
    )
    nc.vector.tensor_scalar(
        out=grid[:, 2:3], in0=partition[:], scalar1=2, scalar2=8, op0=ALU.logical_shift_left, op1=ALU.bitwise_and
    )
    column = pool.tile([P, GROUPS], F32)
    nc.vector.tensor_tensor(out=column[:], in0=group[:], in1=grid[:, 2:3].to_broadcast([P, GROUPS]), op=ALU.add)

    width = PLACES * FREQS
    product = pool.tile([P, PLACES, FREQS], F32)
    nc.vector.tensor_tensor(
        out=product[:, :2, :], in0=grid[:, :2].unsqueeze(2).to_broadcast([P, 2, FREQS]), in1=slope[:, :2, :], op=ALU.mult
    )
    nc.vector.tensor_tensor(
        out=product[:, 2:, :],
        in0=column[:].unsqueeze(2).to_broadcast([P, GROUPS, FREQS]),
        in1=slope[:, 2:, :],
        op=ALU.mult,
    )
    units = pool.tile([P, 4, PLACES, FREQS], F32)
    nc.vector.tensor_tensor(
        out=units[:],
        in0=product[:].unsqueeze(1).to_broadcast([P, 4, PLACES, FREQS]),
        in1=start[:].rearrange("p c e f -> p (c e) f").unsqueeze(2).to_broadcast([P, 4, PLACES, FREQS]),
        op=ALU.add,
    )
    flat = units[:].rearrange("p s r f -> p s (r f)")
    shifted = pool.tile([P, 4, width], F32)
    nc.vector.tensor_scalar(
        out=shifted[:], in0=flat, scalar1=1.0 / HALF_TURN, scalar2=ROUND_MAGIC, op0=ALU.mult, op1=ALU.add
    )
    half_turns = pool.tile([P, 4, width], I32)
    nc.vector.tensor_scalar(out=half_turns[:], in0=shifted[:], scalar1=ROUND_MAGIC, scalar2=None, op0=ALU.subtract)
    rest = pool.tile([P, 4, width], F32)
    nc.vector.scalar_tensor_tensor(
        out=rest[:], in0=half_turns[:], scalar=-float(HALF_TURN), in1=flat, op0=ALU.mult, op1=ALU.add
    )
    sine = pool.tile([P, 4, width], F32)
    nc.scalar.activation(out=sine[:], in_=rest[:], func=ACT.Sin, scale=math.pi / HALF_TURN)
    odd = pool.tile([P, 4, width], I32)
    nc.vector.tensor_scalar(out=odd[:], in0=half_turns[:], scalar1=1, scalar2=None, op0=ALU.bitwise_and)
    sign = pool.tile([P, 4, width], F32)
    nc.vector.tensor_scalar(out=sign[:], in0=odd[:], scalar1=-2.0, scalar2=1.0, op0=ALU.mult, op1=ALU.add)

    tables = pool.tile([P, GROUPS // 2, 2, 2, ROTATED], F32)
    for c in range(2):
        pairs = tables[:, :, c].rearrange("p m a (i e) -> p m a i e", e=2)
        factors = [values[:, 2 * c : 2 * c + 2, :].rearrange("p e w -> p w e") for values in (sine, sign)]
        shape = [P, GROUPS // 2, SHARED_PAIRS, 2]
        for a in range(2):
            nc.vector.tensor_tensor(
                out=pairs[:, :, a, :SHARED_PAIRS, :],
                in0=factors[0][:, :SHARED_PAIRS, :].unsqueeze(1).to_broadcast(shape),
                in1=factors[1][:, :SHARED_PAIRS, :].unsqueeze(1).to_broadcast(shape),
                op=ALU.mult,
            )
        nc.vector.tensor_tensor(
            out=pairs[:, :, :, SHARED_PAIRS:, :],
            in0=factors[0][:, SHARED_PAIRS:, :].rearrange("p (m a f) e -> p m a f e", a=2, f=FREQS),
            in1=factors[1][:, SHARED_PAIRS:, :].rearrange("p (m a f) e -> p m a f e", a=2, f=FREQS),
            op=ALU.mult,
        )
    return tables


def tile_attention_pa_kernel(tc, x, Wqkv_words, Wqkv_scales, out_0, out_1, out_2):
    nc = tc.nc
    outs = (out_0, out_1, out_2)
    with ExitStack() as ctx:
        keep = ctx.enter_context(tc.tile_pool(name="keep", bufs=1))
        regroup = ctx.enter_context(tc.tile_pool(name="regroup", bufs=4))
        rotated_results = ctx.enter_context(tc.tile_pool(name="rotated_results", bufs=6))
        plain_results = ctx.enter_context(tc.tile_pool(name="plain_results", bufs=4))
        crosses = ctx.enter_context(tc.tile_pool(name="crosses", bufs=6))
        psum = ctx.enter_context(tc.psum_pool(name="psum", bufs=8))

        x_rows = {}
        x_codes = keep.tile([P, GROUPS, PASSES * P], U32, align_bytes=64)
        x_scales = keep.tile([P, GROUPS, PASSES * P], U8, align_bytes=64)
        w_codes = keep.tile([P, PASSES, COLUMNS], U32, align_bytes=64)
        w_scales = keep.tile([P, PASSES, COLUMNS], U8, align_bytes=64)
        first_scales = keep.tile([P, PASSES, FIRST_COLUMNS], U8, align_bytes=64)

        zeros = keep.tile([P, BANK_WORDS], BF16)
        nc.vector.memset(zeros[:], 0.0)
        nc.vector.memset(first_scales[:].bitcast(I32), 0)

        identity = keep.tile([P, P], F32)
        make_identity(nc, identity[:])

        def load_x(groups):
            count = groups.stop - groups.start
            rows = keep.tile([P, count, CHANNELS], BF16, name="x_rows%d" % groups.start)
            nc.sync.dma_start(
                out=rows[:].rearrange("p j k -> p (j k)"),
                in_=x.rearrange("b (r j) k -> r b (j k)", j=GROUPS)[
                    :, :, groups.start * CHANNELS : groups.stop * CHANNELS
                ],
            )
            for a in range(count):
                x_rows[groups.start + a] = rows[:, a, :]

        def load_scales(planes, first_column, columns):
            words = slice(first_column // 4, (first_column + columns) // 4)
            rows = Wqkv_scales.bitcast(I32).rearrange("g q n -> q g n")
            for r in range(4):
                nc.sync.dma_start(out=planes[:].bitcast(I32)[r:P:32, :, :], in_=rows[r:16:4, :, words])

        def scale_plane(g, cols):
            if cols.start >= FIRST_COLUMN and cols.stop <= FIRST_COLUMN + FIRST_COLUMNS:
                return first_scales[:, g, cols.start - FIRST_COLUMN : cols.stop - FIRST_COLUMN]
            return w_scales[:, g, cols]

        def head_columns(which, first_head, heads):
            first = (which * HEADS + first_head) * HEAD_DIM
            return slice(first, first + heads * HEAD_DIM)

        def load_w_codes(first_column, columns):
            words = Wqkv_words.rearrange("g p n t -> g p (n t)").bitcast(I32).rearrange("g p n -> p g n")
            cols = slice(first_column, first_column + columns)
            nc.sync.dma_start(out=w_codes[:, :, cols].bitcast(I32), in_=words[:, :, cols])

        load_x(slice(0, 2))
        load_x(slice(2, 4))
        load_x(slice(4, 6))
        load_x(slice(6, 8))
        tables = build_rotation_tables(nc, keep)

        nc.gpsimd.memset(w_scales[:].bitcast(F32), 0.0)
        load_scales(first_scales, FIRST_COLUMN, FIRST_COLUMNS)
        load_w_codes(FIRST_COLUMN, FIRST_COLUMNS)
        load_w_codes(0, 8 * HEAD_DIM)
        load_scales(w_scales, 0, COLUMNS)
        load_w_codes(FIRST_COLUMN + FIRST_COLUMNS, COLUMNS - FIRST_COLUMN - FIRST_COLUMNS)
        load_w_codes(8 * HEAD_DIM, FIRST_COLUMN - 8 * HEAD_DIM)

        def transpose_group(j):
            words = x_rows[j].bitcast(F32)
            bank = psum.tile([P, PASSES, 2, P], F32, tag="bank", name="x_bank")
            for g in range(PASSES):
                for u in range(2):
                    pass_words = slice(g * WORDS_PER_PASS + u, (g + 1) * WORDS_PER_PASS, 2)
                    nc.tensor.transpose(bank[:, g, u, :], words[:, pass_words], identity[:])
            grouped = regroup.tile([P, PASSES, P, PACK], BF16, align_bytes=64, name="grouped")
            nc.scalar.copy(out=grouped[:].bitcast(F32), in_=bank[:].rearrange("p g u n -> p g n u"))
            return grouped

        def warm_up(moving, count):
            bank = psum.tile([P, BANK_WORDS], F32, tag="bank", name="warm_bank")
            for i in range(count):
                nc.tensor.matmul(bank[:], lhsT=zeros[:, :P], rhs=moving, start=True, stop=True)

        def quantise_group(j, grouped):
            nc.vector.quantize_mx(
                out=x_codes[:, j, :].bitcast(FP8X4),
                scales=x_scales[:, j, :],
                in_=grouped[:].rearrange("p g n t -> p (g n t)"),
            )

        def fill_bank(block, first_group):
            which, first_head, heads, groups_per_add, vector_adds = block["spec"]
            groups_per_bank = BANK_HEADS // heads
            cols = head_columns(which, first_head, heads)
            if first_group == 0:
                pool = plain_results if which == V else rotated_results
                block["staged"] = pool.tile([P, heads, GROUPS, HEAD_DIM], F32, name="staged")
            staged = block["staged"]
            acc = psum.tile([P, groups_per_bank, heads, HEAD_DIM], F32, tag="bank", name="acc")
            for a in range(groups_per_bank):
                for g in range(PASSES):
                    tokens = slice(g * P, (g + 1) * P)
                    nc.tensor.matmul_mx(
                        out=acc[:, a].rearrange("p h d -> p (h d)"),
                        lhsT=x_codes[:, first_group + a, tokens].bitcast(FP8X4),
                        lhsT_scale=x_scales[:, first_group + a, tokens],
                        rhs=w_codes[:, g, cols].bitcast(FP8X4),
                        rhs_scale=scale_plane(g, cols),
                        start=(g == 0),
                        stop=(g == PASSES - 1),
                    )
            if which != V:
                place = first_group % groups_per_add
                if place == 0:
                    block["products"] = crosses.tile([P, 2, groups_per_add, heads, ROTATED], F32, name="products")
                products = block["products"]
                shape = [P, 2, groups_per_bank, heads, ROTATED]
                of_groups = tables[:, first_group // 2, :, first_group % 2 : first_group % 2 + groups_per_bank, :]
                nc.vector.tensor_tensor(
                    out=products[:, :, place : place + groups_per_bank],
                    in0=acc[:, :, :, :ROTATED].unsqueeze(1).to_broadcast(shape),
                    in1=of_groups.unsqueeze(3).to_broadcast(shape),
                    op=ALU.mult,
                )
            return partial(empty_bank, block, first_group, acc)

        def empty_bank(block, first_group, acc):
            which, first_head, heads, groups_per_add, vector_adds = block["spec"]
            groups_per_bank = BANK_HEADS // heads
            last_group = first_group + groups_per_bank - 1
            staged = block["staged"]
            target = staged[:, :, first_group : last_group + 1, :].rearrange("p h a d -> p a h d")
            if which == V:
                nc.scalar.copy(out=target, in_=acc[:])
            else:
                nc.scalar.copy(out=target[:, :, :, ROTATED:], in_=acc[:, :, :, ROTATED:])
                if (last_group + 1) % groups_per_add == 0:
                    adder = nc.vector if vector_adds else nc.gpsimd
                    joined = slice(last_group + 1 - groups_per_add, last_group + 1)
                    products = block["products"]
                    by_pairs = "p a h (i e) -> p a h i e"
                    adder.tensor_tensor(
                        out=staged[:, :, joined, :ROTATED].rearrange("p h a d -> p a h d").rearrange(by_pairs, e=2),
                        in0=products[:, 0].rearrange(by_pairs, e=2),
                        in1=products[:, 1].rearrange(by_pairs, e=2)[:, :, :, :, ::-1],
                        op=ALU.add,
                    )
            if last_group == GROUPS - 1:
                queue = nc.scalar if which == V else nc.sync
                for b in range(BATCH):
                    queue.dma_start(
                        out=outs[which][b, first_head : first_head + heads].rearrange(
                            "h (r j) d -> r h (j d)", j=GROUPS
                        ),
                        in_=staged[b:P:BATCH].rearrange("p h j d -> p h (j d)"),
                    )

        def block_steps(*spec):
            block = {"spec": spec}
            return [partial(fill_bank, block, j) for j in range(0, GROUPS, BANK_HEADS // spec[2])]

        rotated_steps = []
        for spec in ROTATED_BLOCKS:
            rotated_steps.extend(block_steps(*spec))
        plain_steps = []
        for spec in PLAIN_BLOCKS:
            plain_steps.extend(block_steps(*spec))

        warm_up(zeros[:], 4)
        grouped_tiles = {}
        for j in range(GROUPS + 1):
            if j == GROUPS // 2:
                warm_up(x_rows[j][:, :BANK_WORDS], 3)
            if j < GROUPS:
                grouped_tiles[j] = transpose_group(j)
            if j > 0:
                quantise_group(j - 1, grouped_tiles[j - 1])
        done = 0
        for step, fill in enumerate(rotated_steps):
            empty_rotated = fill()
            due = step + 1 if step < PLAIN_HEAD else PLAIN_HEAD + (step + 1 - PLAIN_HEAD) // 2
            for plain in plain_steps[done:due]:
                plain()()
            done = due
            empty_rotated()
